import numpy as np
import ml_dtypes


def mxq(x, axis, fmt="e4m3"):
    dtype, down = {"e4m3": (ml_dtypes.float8_e4m3fn, 7), "e5m2": (ml_dtypes.float8_e5m2, 14)}[fmt]
    v = np.moveaxis(np.asarray(x, np.float32).astype(ml_dtypes.bfloat16).astype(np.float64), axis, -1)
    blocks = v.reshape(v.shape[:-1] + (-1, 32))
    amax = np.abs(blocks).max(-1, keepdims=True)
    byte = np.maximum(np.where(amax > 0, np.frexp(amax)[1] - 1 + 127, 0) - down, 1)
    scale = np.exp2(byte - 127.0)
    codes = (blocks / scale).astype(np.float32).astype(dtype).astype(np.float64)
    return np.moveaxis((codes * scale).reshape(v.shape), -1, axis)


WIDE = False


def mx_kscale(k):
    if not WIDE:
        return np.ones(k)
    levels = np.array([10, -10, 5, -5, 0])
    a = np.random.permutation(np.resize(levels, k // 512 * 4)).reshape(k // 512, 4)
    idx = np.arange(k)
    return np.exp2(a[idx // 512, idx % 128 // 32])


BF16 = ml_dtypes.bfloat16


def bf(x):
    return np.asarray(x, np.float32).astype(BF16)


def f64(x):
    return np.asarray(x).astype(np.float64)


B, N, D = 4, 1024, 512


def setup_inputs():
    s = mx_kscale(D)
    m = np.random.uniform(0.25, 1.75, (B, N, 1))
    return {"q": bf(np.random.standard_normal((B, N, D)) * 3.0 * m),
            "k": bf(np.random.standard_normal((B, N, D)) * 3.0 * m),
            "x": bf(np.random.standard_normal((B, N, D)) * m * s),
            "Wv": bf(np.random.standard_normal((D, D)) * 3.0 / np.sqrt(D) / s[None, :])}


def reference(q, k, x, Wv):
    q, k = f64(q), f64(k)
    v = mxq(f64(x), 2, "e4m3") @ mxq(f64(Wv), 1, "e4m3").T
    qk = mxq(q, 2, "e4m3") @ mxq(k, 2, "e4m3").transpose(0, 2, 1)
    d2 = (q * q).sum(-1)[:, :, None] + (k * k).sum(-1)[:, None, :] - 2.0 * qk
    sc = np.sqrt(np.maximum(d2, 0.0)) / np.sqrt(D)
    e = np.exp(sc - sc.max(-1, keepdims=True))
    return (mxq(e, 2, "e4m3") @ mxq(v, 1, "e4m3")) / e.sum(-1, keepdims=True)

@@ -1,0 +1,287 @@
+from contextlib import ExitStack
+
+import concourse.masks as masks
+import concourse.mybir as mybir
+
+FP8X4 = mybir.dt.float8_e4m3fn_x4
+BF16 = mybir.dt.bfloat16
+F32 = mybir.dt.float32
+U32 = mybir.dt.uint32
+U8 = mybir.dt.uint8
+ACT = mybir.ActivationFunctionType
+ALU = mybir.AluOpType
+
+B, N, D = 4, 1024, 512
+P = 128
+PACK = 4
+K_PASS = P * PACK
+TILES = N // P
+KEY_PASSES = N // K_PASS
+BANK = 512
+HALVES = N // BANK
+
+FLOPS = 2 * B * N * D * D + 2 * 2 * B * N * N * D
+
+
+def load_tokens(nc, raw_pool, rows, n_tiles):
+    raw = raw_pool.tile([P, n_tiles, D], BF16, tag="raw")
+    nc.sync.dma_start(
+        out=raw[:].rearrange("p (g t) d -> p g t d", t=PACK),
+        in_=rows.rearrange("(g p t) d -> p g t d", p=P, t=PACK),
+    )
+    return raw
+
+
+def quantise_along_features(nc, pools, ident_words, raw, n_tiles, codes, scales):
+    tokens = n_tiles * P
+    grouped = pools["grouped"].tile([P, tokens * PACK], BF16, tag="grouped", align_bytes=64)
+    grouped_words = grouped[:].bitcast(F32).rearrange("p (c u) -> p c u", u=2)
+    for pair in range(n_tiles // 2):
+        turned = pools["psum_words"].tile([P, 2, 2 * P], F32, tag="turned")
+        for a in range(2):
+            words = raw[:, 2 * pair + a, :].bitcast(F32)
+            for u in range(2):
+                nc.tensor.transpose(
+                    turned[:, u, a * P : (a + 1) * P], words[:, u * P : (u + 1) * P], ident_words[:]
+                )
+        nc.vector.tensor_copy(
+            out=grouped_words[:, pair * 2 * P : (pair + 1) * 2 * P, :],
+            in_=turned[:].rearrange("p u c -> p c u"),
+        )
+    nc.vector.quantize_mx(
+        out=codes.bitcast(FP8X4),
+        scales=scales,
+        in_=grouped[:],
+    )
+
+
+def sums_of_squares(nc, pools, raw, sums):
+    for T in range(TILES):
+        squares = pools["scratch"].tile([P, D], BF16, tag="squares")
+        nc.scalar.activation(
+            out=squares[:], in_=raw[:, T, :], func=ACT.Square, accum_out=sums[:, T : T + 1]
+        )
+
+
+def tile_attention_pa_t_kernel(tc, q, k, x, Wv, out):
+    nc = tc.nc
+    with ExitStack() as ctx:
+        pools = {
+            "const": ctx.enter_context(tc.tile_pool(name="const", bufs=1)),
+            "raw": ctx.enter_context(tc.tile_pool(name="raw", bufs=4)),
+            "grouped": ctx.enter_context(tc.tile_pool(name="grouped", bufs=2)),
+            "operands": ctx.enter_context(tc.tile_pool(name="operands", bufs=2)),
+            "scratch": ctx.enter_context(tc.tile_pool(name="scratch", bufs=2)),
+            "stats": ctx.enter_context(tc.tile_pool(name="stats", bufs=2)),
+            "scores": ctx.enter_context(tc.tile_pool(name="scores", bufs=12)),
+            "weights": ctx.enter_context(tc.tile_pool(name="weights", bufs=4)),
+            "results": ctx.enter_context(tc.tile_pool(name="results", bufs=2)),
+            "psum_words": ctx.enter_context(tc.psum_pool(name="psum_words", bufs=2)),
+            "psum_values": ctx.enter_context(tc.psum_pool(name="psum_values", bufs=1)),
+            "psum_scores": ctx.enter_context(tc.psum_pool(name="psum_scores", bufs=2)),
+            "psum_weights": ctx.enter_context(tc.psum_pool(name="psum_weights", bufs=2)),
+            "psum_results": ctx.enter_context(tc.psum_pool(name="psum_results", bufs=1)),
+        }
+
+        ident_words = pools["const"].tile([P, P], F32)
+        masks.make_identity(nc, ident_words[:])
+        ident_bf16 = pools["const"].tile([P, P], BF16)
+        masks.make_identity(nc, ident_bf16[:])
+
+        wv_codes = pools["const"].tile([P, D], U32, align_bytes=64)
+        wv_scales = pools["const"].tile([P, D], U8, align_bytes=64)
+
+        def prepare(b):
+            ready = {}
+            k_raw = load_tokens(nc, pools["raw"], k[b], TILES)
+            q_raw = load_tokens(nc, pools["raw"], q[b], TILES)
+            if b == 0:
+                wv_raw = pools["raw"].tile([P, D // P, D], BF16, tag="raw")
+                nc.sync.dma_start(out=wv_raw[:], in_=Wv.rearrange("(t p) f -> p t f", p=P))
+            x_raw = load_tokens(nc, pools["raw"], x[b], TILES)
+
+            def operand(name, raw):
+                codes = pools["operands"].tile([P, N], U32, tag=name + "_codes", align_bytes=64)
+                scales = pools["operands"].tile([P, N], U8, tag=name + "_scales", align_bytes=64)
+                quantise_along_features(nc, pools, ident_words, raw, TILES, codes[:], scales[:])
+                return codes, scales
+
+            ready["k"] = operand("k", k_raw)
+            kk = pools["stats"].tile([P, TILES], F32, tag="kk")
+            sums_of_squares(nc, pools, k_raw, kk)
+            ready["q"] = operand("q", q_raw)
+            qq = pools["stats"].tile([P, TILES], F32, tag="qq")
+            sums_of_squares(nc, pools, q_raw, qq)
+            neg_qq = pools["stats"].tile([P, TILES], F32, tag="neg_qq")
+            nc.vector.tensor_scalar_mul(neg_qq[:], qq[:], -1.0)
+            qq_over_d = pools["stats"].tile([P, TILES], F32, tag="qq_over_d")
+            nc.vector.tensor_scalar_mul(qq_over_d[:], qq[:], 1.0 / D)
+            ready["qq"], ready["neg_qq"], ready["qq_over_d"] = qq, neg_qq, qq_over_d
+
+            kk_rows = pools["operands"].tile([P, N], F32, tag="kk_rows")
+            for h in range(HALVES):
+                spread = pools["psum_values"].tile([P, PACK, P], F32, tag="values")
+                for t in range(PACK):
+                    T = h * PACK + t
+                    nc.tensor.transpose(
+                        spread[:, t, :], kk[:, T : T + 1].to_broadcast([P, P]), ident_words[:]
+                    )
+                nc.scalar.copy(
+                    out=kk_rows[:, h * BANK : (h + 1) * BANK],
+                    in_=spread[:].rearrange("p t c -> p (t c)"),
+                )
+            ready["kk_rows"] = kk_rows
+
+            if b == 0:
+                quantise_along_features(
+                    nc, pools, ident_words, wv_raw, D // P, wv_codes[:], wv_scales[:]
+                )
+            x_codes, x_scales = operand("x", x_raw)
+            v_shape = [P, KEY_PASSES, D, PACK]
+            v_grouped = pools["grouped"].tile(v_shape, BF16, tag="grouped", align_bytes=64)
+            for g in range(KEY_PASSES):
+                for c in range(D // P):
+                    values = pools["psum_values"].tile([P, PACK, P], F32, tag="values")
+                    for t in range(PACK):
+                        T = g * PACK + t
+                        nc.tensor.matmul_mx(
+                            out=values[:, t, :],
+                            lhsT=x_codes[:, T * P : (T + 1) * P].bitcast(FP8X4),
+                            lhsT_scale=x_scales[:, T * P : (T + 1) * P],
+                            rhs=wv_codes[:, c * P : (c + 1) * P].bitcast(FP8X4),
+                            rhs_scale=wv_scales[:, c * P : (c + 1) * P],
+                            start=True,
+                            stop=True,
+                        )
+                    nc.scalar.copy(
+                        out=v_grouped[:, g, c * P : (c + 1) * P, :],
+                        in_=values[:].rearrange("p t d -> p d t"),
+                    )
+            v_codes = pools["operands"].tile([P, KEY_PASSES, D], U32, tag="v_codes", align_bytes=64)
+            v_scales = pools["operands"].tile([P, KEY_PASSES, D], U8, tag="v_scales", align_bytes=64)
+            nc.vector.quantize_mx(
+                out=v_codes[:].rearrange("p g d -> p (g d)").bitcast(FP8X4),
+                scales=v_scales[:].rearrange("p g d -> p (g d)"),
+                in_=v_grouped[:].rearrange("p g d t -> p (g d t)"),
+            )
+            ready["v"] = (v_codes, v_scales)
+            return ready
+
+        def distances(ready):
+            q_codes, q_scales = ready["q"]
+            k_codes, k_scales = ready["k"]
+            peak = pools["stats"].tile([P, TILES], F32, tag="peak")
+            rows = []
+            for T in range(TILES):
+                s = pools["scores"].tile([P, N], F32, tag="s")
+                for h in range(HALVES):
+                    qk = pools["psum_scores"].tile([P, BANK], F32, tag="qk")
+                    nc.tensor.matmul_mx(
+                        out=qk[:],
+                        lhsT=q_codes[:, T * P : (T + 1) * P].bitcast(FP8X4),
+                        lhsT_scale=q_scales[:, T * P : (T + 1) * P],
+                        rhs=k_codes[:, h * BANK : (h + 1) * BANK].bitcast(FP8X4),
+                        rhs_scale=k_scales[:, h * BANK : (h + 1) * BANK],
+                        start=True,
+                        stop=True,
+                    )
+                    nc.vector.scalar_tensor_tensor(
+                        out=s[:, h * BANK : (h + 1) * BANK],
+                        in0=qk[:],
+                        scalar=-2.0,
+                        in1=ready["kk_rows"][:, h * BANK : (h + 1) * BANK],
+                        op0=ALU.mult,
+                        op1=ALU.add,
+                    )
+                nc.vector.tensor_scalar(
+                    out=s[:],
+                    in0=s[:],
+                    scalar1=ready["neg_qq"][:, T : T + 1],
+                    scalar2=None,
+                    op0=ALU.max,
+                    op1=ALU.max,
+                    accum_out=peak[:, T : T + 1],
+                )
+                nc.scalar.activation(
+                    out=s[:],
+                    in_=s[:],
+                    func=ACT.Sqrt,
+                    bias=ready["qq_over_d"][:, T : T + 1],
+                    scale=1.0 / D,
+                )
+                rows.append(s)
+            largest_d2 = pools["stats"].tile([P, TILES], F32, tag="largest_d2")
+            nc.vector.tensor_tensor(out=largest_d2[:], in0=peak[:], in1=ready["qq"][:], op=ALU.add)
+            row_max = pools["stats"].tile([P, TILES], F32, tag="row_max")
+            nc.scalar.activation(out=row_max[:], in_=largest_d2[:], func=ACT.Sqrt, scale=1.0 / D)
+            neg_row_max = pools["stats"].tile([P, TILES], F32, tag="neg_row_max")
+            nc.scalar.mul(neg_row_max[:], row_max[:], -1.0)
+            return rows, neg_row_max
+
+        def attend(b, ready, rows, neg_row_max):
+            v_codes, v_scales = ready["v"]
+            out_tiles = out[b].rearrange("(g p t) d -> p g t d", p=P, t=PACK)
+            row_sum = pools["stats"].tile([P, TILES], F32, tag="row_sum")
+            one_over_sum = pools["stats"].tile([P, TILES], F32, tag="one_over_sum")
+            for T in range(TILES):
+                e = pools["weights"].tile([P, N], BF16, tag="e")
+                nc.scalar.activation(
+                    out=e[:],
+                    in_=rows[T][:],
+                    func=ACT.Exp,
+                    bias=neg_row_max[:, T : T + 1],
+                    scale=1.0,
+                    accum_out=row_sum[:, T : T + 1],
+                )
+                nc.vector.reciprocal(one_over_sum[:, T : T + 1], row_sum[:, T : T + 1])
+
+                e_turned = pools["psum_weights"].tile([P, TILES, P], BF16, tag="e_turned")
+                for J in range(TILES):
+                    nc.tensor.transpose(e_turned[:, J, :], e[:, J * P : (J + 1) * P], ident_bf16[:])
+                e_shape = [P, KEY_PASSES, P, PACK]
+                e_grouped = pools["weights"].tile(e_shape, BF16, tag="e_grouped", align_bytes=64)
+                nc.vector.tensor_copy(
+                    out=e_grouped[:], in_=e_turned[:].rearrange("p (g t) i -> p g i t", t=PACK)
+                )
+                e_codes = pools["weights"].tile([P, KEY_PASSES, P], U32, tag="e_codes", align_bytes=64)
+                e_scales = pools["weights"].tile([P, KEY_PASSES, P], U8, tag="e_scales", align_bytes=64)
+                nc.vector.quantize_mx(
+                    out=e_codes[:].rearrange("p g i -> p (g i)").bitcast(FP8X4),
+                    scales=e_scales[:].rearrange("p g i -> p (g i)"),
+                    in_=e_grouped[:].rearrange("p g i t -> p (g i t)"),
+                )
+
+                summed = pools["psum_results"].tile([P, D], F32, tag="summed")
+                for g in range(KEY_PASSES):
+                    nc.tensor.matmul_mx(
+                        out=summed[:],
+                        lhsT=e_codes[:, g, :].bitcast(FP8X4),
+                        lhsT_scale=e_scales[:, g, :],
+                        rhs=v_codes[:, g, :].bitcast(FP8X4),
+                        rhs_scale=v_scales[:, g, :],
+                        start=(g == 0),
+                        stop=(g == KEY_PASSES - 1),
+                    )
+                g, t = divmod(T, PACK)
+                if t == 0:
+                    result = pools["results"].tile([P, PACK, D], F32, tag="result")
+                if T % 2 == 0:
+                    nc.scalar.activation(
+                        out=result[:, t, :],
+                        in_=summed[:],
+                        func=ACT.Copy,
+                        scale=one_over_sum[:, T : T + 1],
+                    )
+                else:
+                    nc.vector.tensor_scalar_mul(
+                        result[:, t, :], summed[:], one_over_sum[:, T : T + 1]
+                    )
+                if t == PACK - 1:
+                    nc.sync.dma_start(out=out_tiles[:, g], in_=result[:])
+
+        ready = prepare(0)
+        for b in range(B):
+            rows, neg_row_max = distances(ready)
+            following = prepare(b + 1) if b + 1 < B else None
+            attend(b, ready, rows, neg_row_max)
+            ready = following

@@ -23,265 +23,372 @@ HALVES = N // BANK
 FLOPS = 2 * B * N * D * D + 2 * 2 * B * N * N * D
 
 
-def load_tokens(nc, raw_pool, rows, n_tiles):
-    raw = raw_pool.tile([P, n_tiles, D], BF16, tag="raw")
+def load_tokens(nc, raw, rows):
     nc.sync.dma_start(
         out=raw[:].rearrange("p (g t) d -> p g t d", t=PACK),
         in_=rows.rearrange("(g p t) d -> p g t d", p=P, t=PACK),
     )
-    return raw
 
 
-def quantise_along_features(nc, pools, ident_words, raw, n_tiles, codes, scales):
-    tokens = n_tiles * P
-    grouped = pools["grouped"].tile([P, tokens * PACK], BF16, tag="grouped", align_bytes=64)
+def turn_words(nc, turned, raw, pair, ident_words):
+    for a in range(2):
+        words = raw[:, 2 * pair + a, :].bitcast(F32)
+        for u in range(2):
+            nc.tensor.transpose(
+                turned[:, u, a * P : (a + 1) * P], words[:, u * P : (u + 1) * P], ident_words[:]
+            )
+
+
+def regroup_words(nc, grouped, turned, pair):
     grouped_words = grouped[:].bitcast(F32).rearrange("p (c u) -> p c u", u=2)
-    for pair in range(n_tiles // 2):
-        turned = pools["psum_words"].tile([P, 2, 2 * P], F32, tag="turned")
-        for a in range(2):
-            words = raw[:, 2 * pair + a, :].bitcast(F32)
-            for u in range(2):
-                nc.tensor.transpose(
-                    turned[:, u, a * P : (a + 1) * P], words[:, u * P : (u + 1) * P], ident_words[:]
-                )
-        nc.vector.tensor_copy(
-            out=grouped_words[:, pair * 2 * P : (pair + 1) * 2 * P, :],
-            in_=turned[:].rearrange("p u c -> p c u"),
-        )
-    nc.vector.quantize_mx(
-        out=codes.bitcast(FP8X4),
-        scales=scales,
-        in_=grouped[:],
+    nc.vector.tensor_copy(
+        out=grouped_words[:, pair * 2 * P : (pair + 1) * 2 * P, :],
+        in_=turned[:].rearrange("p u c -> p c u"),
     )
 
 
-def sums_of_squares(nc, pools, raw, sums):
-    for T in range(TILES):
-        squares = pools["scratch"].tile([P, D], BF16, tag="squares")
-        nc.scalar.activation(
-            out=squares[:], in_=raw[:, T, :], func=ACT.Square, accum_out=sums[:, T : T + 1]
-        )
+def quantise_columns(nc, codes, scales, grouped, first, count):
+    nc.vector.quantize_mx(
+        out=codes[:, first : first + count].bitcast(FP8X4),
+        scales=scales[:, first : first + count],
+        in_=grouped[:, first * PACK : (first + count) * PACK],
+    )
+
+
+def square_sum(nc, scratch_pool, sums, raw, T):
+    squares = scratch_pool.tile([P, D], BF16, tag="squares")
+    nc.scalar.activation(
+        out=squares[:], in_=raw[:, T, :], func=ACT.Square, accum_out=sums[:, T : T + 1]
+    )
 
 
 def tile_attention_pa_t_kernel(tc, q, k, x, Wv, out):
     nc = tc.nc
+    inputs = {"k": k, "q": q, "x": x}
     with ExitStack() as ctx:
-        pools = {
-            "const": ctx.enter_context(tc.tile_pool(name="const", bufs=1)),
-            "raw": ctx.enter_context(tc.tile_pool(name="raw", bufs=4)),
-            "grouped": ctx.enter_context(tc.tile_pool(name="grouped", bufs=2)),
-            "operands": ctx.enter_context(tc.tile_pool(name="operands", bufs=2)),
-            "scratch": ctx.enter_context(tc.tile_pool(name="scratch", bufs=2)),
-            "stats": ctx.enter_context(tc.tile_pool(name="stats", bufs=2)),
-            "scores": ctx.enter_context(tc.tile_pool(name="scores", bufs=12)),
-            "weights": ctx.enter_context(tc.tile_pool(name="weights", bufs=4)),
-            "results": ctx.enter_context(tc.tile_pool(name="results", bufs=2)),
-            "psum_words": ctx.enter_context(tc.psum_pool(name="psum_words", bufs=2)),
-            "psum_values": ctx.enter_context(tc.psum_pool(name="psum_values", bufs=1)),
-            "psum_scores": ctx.enter_context(tc.psum_pool(name="psum_scores", bufs=2)),
-            "psum_weights": ctx.enter_context(tc.psum_pool(name="psum_weights", bufs=2)),
-            "psum_results": ctx.enter_context(tc.psum_pool(name="psum_results", bufs=1)),
-        }
+        const_pool = ctx.enter_context(tc.tile_pool(name="const", bufs=1))
+        raw_pool = ctx.enter_context(tc.tile_pool(name="raw", bufs=2))
+        operand_pool = ctx.enter_context(tc.tile_pool(name="operands", bufs=1))
+        scratch_pool = ctx.enter_context(tc.tile_pool(name="scratch", bufs=2))
+        stats_pool = ctx.enter_context(tc.tile_pool(name="stats", bufs=2))
+        score_pool = ctx.enter_context(tc.tile_pool(name="scores", bufs=TILES))
+        e_pool = ctx.enter_context(tc.tile_pool(name="e", bufs=TILES))
+        weight_pool = ctx.enter_context(tc.tile_pool(name="weights", bufs=3))
+        result_pool = ctx.enter_context(tc.tile_pool(name="results", bufs=2))
+        psum_staging = ctx.enter_context(tc.psum_pool(name="psum_staging", bufs=2))
+        psum_sums = ctx.enter_context(tc.psum_pool(name="psum_sums", bufs=4))
+        psum_turned = ctx.enter_context(tc.psum_pool(name="psum_turned", bufs=2))
+        ctx.enter_context(tc.manual_schedule())
 
-        ident_words = pools["const"].tile([P, P], F32)
+        ident_words = const_pool.tile([P, P], F32)
         masks.make_identity(nc, ident_words[:])
-        ident_bf16 = pools["const"].tile([P, P], BF16)
+        ident_bf16 = const_pool.tile([P, P], BF16)
         masks.make_identity(nc, ident_bf16[:])
 
-        wv_codes = pools["const"].tile([P, D], U32, align_bytes=64)
-        wv_scales = pools["const"].tile([P, D], U8, align_bytes=64)
+        raw = {}
+        operand = {}
+        kk_rows = {}
+        stat = {}
+        banks = {}
+        rows = {}
+        weights = {}
+        results = {}
 
-        def prepare(b):
-            ready = {}
-            k_raw = load_tokens(nc, pools["raw"], k[b], TILES)
-            q_raw = load_tokens(nc, pools["raw"], q[b], TILES)
-            if b == 0:
-                wv_raw = pools["raw"].tile([P, D // P, D], BF16, tag="raw")
-                nc.sync.dma_start(out=wv_raw[:], in_=Wv.rearrange("(t p) f -> p t f", p=P))
-            x_raw = load_tokens(nc, pools["raw"], x[b], TILES)
+        def start_batch(b):
+            for name in ("k", "q", "x"):
+                rows_in = raw_pool.tile([P, TILES, D], BF16, tag=name + "_raw")
+                load_tokens(nc, rows_in, inputs[name][b])
+                raw[(name, b)] = rows_in
 
-            def operand(name, raw):
-                codes = pools["operands"].tile([P, N], U32, tag=name + "_codes", align_bytes=64)
-                scales = pools["operands"].tile([P, N], U8, tag=name + "_scales", align_bytes=64)
-                quantise_along_features(nc, pools, ident_words, raw, TILES, codes[:], scales[:])
-                return codes, scales
+        def new_operand(name, b, columns):
+            grouped = operand_pool.tile([P, columns * PACK], BF16, tag=name + "_grouped", align_bytes=64)
+            codes = operand_pool.tile([P, columns], U32, tag=name + "_codes", align_bytes=64)
+            scales = operand_pool.tile([P, columns], U8, tag=name + "_scales", align_bytes=64)
+            operand[(name, b)] = (grouped, codes, scales)
 
-            ready["k"] = operand("k", k_raw)
-            kk = pools["stats"].tile([P, TILES], F32, tag="kk")
-            sums_of_squares(nc, pools, k_raw, kk)
-            ready["q"] = operand("q", q_raw)
-            qq = pools["stats"].tile([P, TILES], F32, tag="qq")
-            sums_of_squares(nc, pools, q_raw, qq)
-            neg_qq = pools["stats"].tile([P, TILES], F32, tag="neg_qq")
-            nc.vector.tensor_scalar_mul(neg_qq[:], qq[:], -1.0)
-            qq_over_d = pools["stats"].tile([P, TILES], F32, tag="qq_over_d")
-            nc.vector.tensor_scalar_mul(qq_over_d[:], qq[:], 1.0 / D)
-            ready["qq"], ready["neg_qq"], ready["qq_over_d"] = qq, neg_qq, qq_over_d
+        def new_stat(name, b):
+            column_per_tile = stats_pool.tile([P, TILES], F32, tag=name)
+            stat[(name, b)] = column_per_tile
+            return column_per_tile
 
-            kk_rows = pools["operands"].tile([P, N], F32, tag="kk_rows")
+
+        def score_passes(b, T):
+            q_codes, q_scales = operand[("q", b)][1:]
+            k_codes, k_scales = operand[("k", b)][1:]
             for h in range(HALVES):
-                spread = pools["psum_values"].tile([P, PACK, P], F32, tag="values")
+                qk = psum_sums.tile([P, BANK], F32, tag="sums")
+                nc.tensor.matmul_mx(
+                    out=qk[:],
+                    lhsT=q_codes[:, T * P : (T + 1) * P].bitcast(FP8X4),
+                    lhsT_scale=q_scales[:, T * P : (T + 1) * P],
+                    rhs=k_codes[:, h * BANK : (h + 1) * BANK].bitcast(FP8X4),
+                    rhs_scale=k_scales[:, h * BANK : (h + 1) * BANK],
+                    start=True,
+                    stop=True,
+                )
+                banks[("qk", b, T, h)] = qk
+
+        def keys_minus_products(b, T):
+            s = score_pool.tile([P, N], F32, tag="s")
+            for h in range(HALVES):
+                nc.vector.scalar_tensor_tensor(
+                    out=s[:, h * BANK : (h + 1) * BANK],
+                    in0=banks[("qk", b, T, h)][:],
+                    scalar=-2.0,
+                    in1=kk_rows[b][:, h * BANK : (h + 1) * BANK],
+                    op0=ALU.mult,
+                    op1=ALU.add,
+                )
+            rows[(b, T)] = s
+
+        def clamp_and_peak(b, T):
+            nc.vector.tensor_scalar(
+                out=rows[(b, T)][:],
+                in0=rows[(b, T)][:],
+                scalar1=stat[("neg_qq", b)][:, T : T + 1],
+                scalar2=None,
+                op0=ALU.max,
+                op1=ALU.max,
+                accum_out=stat[("peak", b)][:, T : T + 1],
+            )
+
+        def square_root(b, T):
+            nc.scalar.activation(
+                out=rows[(b, T)][:],
+                in_=rows[(b, T)][:],
+                func=ACT.Sqrt,
+                bias=stat[("qq_over_d", b)][:, T : T + 1],
+                scale=1.0 / D,
+            )
+
+        def row_maxima(b):
+            largest_d2 = new_stat("largest_d2", b)
+            nc.vector.tensor_tensor(
+                out=largest_d2[:], in0=stat[("peak", b)][:], in1=stat[("qq", b)][:], op=ALU.add
+            )
+            row_max = new_stat("row_max", b)
+            nc.scalar.activation(out=row_max[:], in_=largest_d2[:], func=ACT.Sqrt, scale=1.0 / D)
+            nc.scalar.mul(new_stat("neg_row_max", b)[:], row_max[:], -1.0)
+
+        def value_passes(b, C):
+            x_codes, x_scales = operand[("x", b)][1:]
+            wv_codes, wv_scales = operand[("wv", 0)][1:]
+            g, c = divmod(C, D // P)
+            if C % 2 == 0:
+                values = psum_staging.tile([P, PACK, P], F32, tag="staging")
+            else:
+                values = psum_turned.tile([P, PACK, P], F32, tag="e_turned")
+            for t in range(PACK):
+                T = g * PACK + t
+                nc.tensor.matmul_mx(
+                    out=values[:, t, :],
+                    lhsT=x_codes[:, T * P : (T + 1) * P].bitcast(FP8X4),
+                    lhsT_scale=x_scales[:, T * P : (T + 1) * P],
+                    rhs=wv_codes[:, c * P : (c + 1) * P].bitcast(FP8X4),
+                    rhs_scale=wv_scales[:, c * P : (c + 1) * P],
+                    start=True,
+                    stop=True,
+                )
+            banks[("values", b, C)] = values
+
+        def round_values(b, C):
+            v_grouped = operand[("v", b)][0]
+            nc.scalar.copy(
+                out=v_grouped[:, C * P * PACK : (C + 1) * P * PACK].rearrange("p (d t) -> p d t", t=PACK),
+                in_=banks[("values", b, C)][:].rearrange("p t d -> p d t"),
+            )
+
+        def quantise_values(b):
+            v_grouped, v_codes, v_scales = operand[("v", b)]
+            quantise_columns(nc, v_codes, v_scales, v_grouped, 0, KEY_PASSES * D)
+
+
+        def exponentials(b, T):
+            e = e_pool.tile([P, N], BF16, tag="e")
+            nc.scalar.activation(
+                out=e[:],
+                in_=rows[(b, T)][:],
+                func=ACT.Exp,
+                bias=stat[("neg_row_max", b)][:, T : T + 1],
+                scale=1.0,
+                accum_out=stat[("row_sum", b)][:, T : T + 1],
+            )
+            weights[("e", b, T)] = e
+
+        def turn_weights(b, T):
+            e = weights[("e", b, T)]
+            e_turned = psum_turned.tile([P, TILES, P], BF16, tag="e_turned")
+            for J in range(TILES):
+                nc.tensor.transpose(e_turned[:, J, :], e[:, J * P : (J + 1) * P], ident_bf16[:])
+            banks[("e_turned", b, T)] = e_turned
+
+        def group_weights(b, T):
+            e_grouped = weight_pool.tile([P, KEY_PASSES * P * PACK], BF16, tag="e_grouped", align_bytes=64)
+            nc.vector.tensor_copy(
+                out=e_grouped[:].rearrange("p (g i t) -> p g i t", g=KEY_PASSES, t=PACK),
+                in_=banks[("e_turned", b, T)][:].rearrange("p (g t) i -> p g i t", t=PACK),
+            )
+            weights[("e_grouped", b, T)] = e_grouped
+            nc.vector.reciprocal(
+                stat[("one_over_sum", b)][:, T : T + 1], stat[("row_sum", b)][:, T : T + 1]
+            )
+
+        def quantise_weights(b, T):
+            e_codes = weight_pool.tile([P, KEY_PASSES * P], U32, tag="e_codes", align_bytes=64)
+            e_scales = weight_pool.tile([P, KEY_PASSES * P], U8, tag="e_scales", align_bytes=64)
+            quantise_columns(nc, e_codes, e_scales, weights[("e_grouped", b, T)], 0, KEY_PASSES * P)
+            weights[("e_codes", b, T)] = (e_codes, e_scales)
+
+        def weighted_sum(b, T):
+            e_codes, e_scales = weights[("e_codes", b, T)]
+            v_codes, v_scales = operand[("v", b)][1:]
+            summed = psum_sums.tile([P, D], F32, tag="sums")
+            for g in range(KEY_PASSES):
+                nc.tensor.matmul_mx(
+                    out=summed[:],
+                    lhsT=e_codes[:, g * P : (g + 1) * P].bitcast(FP8X4),
+                    lhsT_scale=e_scales[:, g * P : (g + 1) * P],
+                    rhs=v_codes[:, g * D : (g + 1) * D].bitcast(FP8X4),
+                    rhs_scale=v_scales[:, g * D : (g + 1) * D],
+                    start=(g == 0),
+                    stop=(g == KEY_PASSES - 1),
+                )
+            banks[("summed", b, T)] = summed
+
+        def divide_and_store(b, T):
+            g, t = divmod(T, PACK)
+            if t == 0:
+                four_tiles = result_pool.tile([P, PACK, D], F32, tag="result")
+                results[(b, g)] = four_tiles
+            nc.scalar.activation(
+                out=results[(b, g)][:, t, :],
+                in_=banks[("summed", b, T)][:],
+                func=ACT.Copy,
+                scale=stat[("one_over_sum", b)][:, T : T + 1],
+            )
+            if t == PACK - 1:
+                out_tiles = out[b].rearrange("(g p t) d -> p g t d", p=P, t=PACK)
+                nc.sync.dma_start(out=out_tiles[:, g], in_=results[(b, g)][:])
+
+        def turn_input_bank(name, b, pair):
+            turned = psum_staging.tile([P, 2, 2 * P], F32, tag="staging")
+            turn_words(nc, turned, raw[(name, b)], pair, ident_words)
+            banks[(name, b, pair)] = turned
+
+        def quantise_input_bank(name, b, pair):
+            grouped, codes, scales = operand[(name, b)]
+            quantise_columns(nc, codes, scales, grouped, pair * 2 * P, 2 * P)
+
+        def spread_key_sums(b):
+            spread_rows = operand_pool.tile([P, N], F32, tag="kk_rows")
+            for h in range(HALVES):
+                spread = psum_staging.tile([P, PACK, P], F32, tag="staging")
                 for t in range(PACK):
                     T = h * PACK + t
                     nc.tensor.transpose(
-                        spread[:, t, :], kk[:, T : T + 1].to_broadcast([P, P]), ident_words[:]
+                        spread[:, t, :],
+                        stat[("kk", b)][:, T : T + 1].to_broadcast([P, P]),
+                        ident_words[:],
                     )
-                nc.scalar.copy(
-                    out=kk_rows[:, h * BANK : (h + 1) * BANK],
+                nc.vector.tensor_copy(
+                    out=spread_rows[:, h * BANK : (h + 1) * BANK],
                     in_=spread[:].rearrange("p t c -> p (t c)"),
                 )
-            ready["kk_rows"] = kk_rows
+            kk_rows[b] = spread_rows
 
-            if b == 0:
-                quantise_along_features(
-                    nc, pools, ident_words, wv_raw, D // P, wv_codes[:], wv_scales[:]
-                )
-            x_codes, x_scales = operand("x", x_raw)
-            v_shape = [P, KEY_PASSES, D, PACK]
-            v_grouped = pools["grouped"].tile(v_shape, BF16, tag="grouped", align_bytes=64)
-            for g in range(KEY_PASSES):
-                for c in range(D // P):
-                    values = pools["psum_values"].tile([P, PACK, P], F32, tag="values")
-                    for t in range(PACK):
-                        T = g * PACK + t
-                        nc.tensor.matmul_mx(
-                            out=values[:, t, :],
-                            lhsT=x_codes[:, T * P : (T + 1) * P].bitcast(FP8X4),
-                            lhsT_scale=x_scales[:, T * P : (T + 1) * P],
-                            rhs=wv_codes[:, c * P : (c + 1) * P].bitcast(FP8X4),
-                            rhs_scale=wv_scales[:, c * P : (c + 1) * P],
-                            start=True,
-                            stop=True,
-                        )
-                    nc.scalar.copy(
-                        out=v_grouped[:, g, c * P : (c + 1) * P, :],
-                        in_=values[:].rearrange("p t d -> p d t"),
-                    )
-            v_codes = pools["operands"].tile([P, KEY_PASSES, D], U32, tag="v_codes", align_bytes=64)
-            v_scales = pools["operands"].tile([P, KEY_PASSES, D], U8, tag="v_scales", align_bytes=64)
-            nc.vector.quantize_mx(
-                out=v_codes[:].rearrange("p g d -> p (g d)").bitcast(FP8X4),
-                scales=v_scales[:].rearrange("p g d -> p (g d)"),
-                in_=v_grouped[:].rearrange("p g d t -> p (g d t)"),
-            )
-            ready["v"] = (v_codes, v_scales)
-            return ready
 
-        def distances(ready):
-            q_codes, q_scales = ready["q"]
-            k_codes, k_scales = ready["k"]
-            peak = pools["stats"].tile([P, TILES], F32, tag="peak")
-            rows = []
+        def valid(b):
+            return 0 <= b < B
+
+        def weights_stage(b, ahead):
+            if valid(ahead):
+                new_stat("kk", ahead)
+            if valid(b):
+                new_stat("row_sum", b)
+                new_stat("one_over_sum", b)
+                for T in range(TILES):
+                    exponentials(b, T)
+                turn_weights(b, 0)
             for T in range(TILES):
-                s = pools["scores"].tile([P, N], F32, tag="s")
-                for h in range(HALVES):
-                    qk = pools["psum_scores"].tile([P, BANK], F32, tag="qk")
-                    nc.tensor.matmul_mx(
-                        out=qk[:],
-                        lhsT=q_codes[:, T * P : (T + 1) * P].bitcast(FP8X4),
-                        lhsT_scale=q_scales[:, T * P : (T + 1) * P],
-                        rhs=k_codes[:, h * BANK : (h + 1) * BANK].bitcast(FP8X4),
-                        rhs_scale=k_scales[:, h * BANK : (h + 1) * BANK],
-                        start=True,
-                        stop=True,
-                    )
-                    nc.vector.scalar_tensor_tensor(
-                        out=s[:, h * BANK : (h + 1) * BANK],
-                        in0=qk[:],
-                        scalar=-2.0,
-                        in1=ready["kk_rows"][:, h * BANK : (h + 1) * BANK],
-                        op0=ALU.mult,
-                        op1=ALU.add,
-                    )
-                nc.vector.tensor_scalar(
-                    out=s[:],
-                    in0=s[:],
-                    scalar1=ready["neg_qq"][:, T : T + 1],
-                    scalar2=None,
-                    op0=ALU.max,
-                    op1=ALU.max,
-                    accum_out=peak[:, T : T + 1],
-                )
-                nc.scalar.activation(
-                    out=s[:],
-                    in_=s[:],
-                    func=ACT.Sqrt,
-                    bias=ready["qq_over_d"][:, T : T + 1],
-                    scale=1.0 / D,
-                )
-                rows.append(s)
-            largest_d2 = pools["stats"].tile([P, TILES], F32, tag="largest_d2")
-            nc.vector.tensor_tensor(out=largest_d2[:], in0=peak[:], in1=ready["qq"][:], op=ALU.add)
-            row_max = pools["stats"].tile([P, TILES], F32, tag="row_max")
-            nc.scalar.activation(out=row_max[:], in_=largest_d2[:], func=ACT.Sqrt, scale=1.0 / D)
-            neg_row_max = pools["stats"].tile([P, TILES], F32, tag="neg_row_max")
-            nc.scalar.mul(neg_row_max[:], row_max[:], -1.0)
-            return rows, neg_row_max
+                if valid(b):
+                    if T + 1 < TILES:
+                        turn_weights(b, T + 1)
+                    group_weights(b, T)
+                    if T >= 1:
+                        quantise_weights(b, T - 1)
+                        weighted_sum(b, T - 1)
+                    if T >= 2:
+                        divide_and_store(b, T - 2)
+                if valid(ahead):
+                    square_sum(nc, scratch_pool, stat[("kk", ahead)], raw[("k", ahead)], T)
 
-        def attend(b, ready, rows, neg_row_max):
-            v_codes, v_scales = ready["v"]
-            out_tiles = out[b].rearrange("(g p t) d -> p g t d", p=P, t=PACK)
-            row_sum = pools["stats"].tile([P, TILES], F32, tag="row_sum")
-            one_over_sum = pools["stats"].tile([P, TILES], F32, tag="one_over_sum")
+        def weights_stage_end(b):
+            quantise_weights(b, TILES - 1)
+            weighted_sum(b, TILES - 1)
+            divide_and_store(b, TILES - 2)
+            divide_and_store(b, TILES - 1)
+
+        def distances_stage(b, ahead):
+            if valid(ahead):
+                new_stat("qq", ahead)
+            if valid(b):
+                new_operand("v", b, KEY_PASSES * D)
+                new_stat("peak", b)
             for T in range(TILES):
-                e = pools["weights"].tile([P, N], BF16, tag="e")
-                nc.scalar.activation(
-                    out=e[:],
-                    in_=rows[T][:],
-                    func=ACT.Exp,
-                    bias=neg_row_max[:, T : T + 1],
-                    scale=1.0,
-                    accum_out=row_sum[:, T : T + 1],
-                )
-                nc.vector.reciprocal(one_over_sum[:, T : T + 1], row_sum[:, T : T + 1])
+                if valid(b):
+                    if T + 1 < TILES:
+                        score_passes(b, T + 1)
+                    value_passes(b, T)
+                    keys_minus_products(b, T)
+                    if T >= 1:
+                        clamp_and_peak(b, T - 1)
+                if valid(ahead):
+                    square_sum(nc, scratch_pool, stat[("qq", ahead)], raw[("q", ahead)], T)
+                if valid(b):
+                    round_values(b, T)
+                    if T >= 2:
+                        square_root(b, T - 2)
+            if valid(b):
+                clamp_and_peak(b, TILES - 1)
+                square_root(b, TILES - 2)
+                square_root(b, TILES - 1)
+                row_maxima(b)
 
-                e_turned = pools["psum_weights"].tile([P, TILES, P], BF16, tag="e_turned")
-                for J in range(TILES):
-                    nc.tensor.transpose(e_turned[:, J, :], e[:, J * P : (J + 1) * P], ident_bf16[:])
-                e_shape = [P, KEY_PASSES, P, PACK]
-                e_grouped = pools["weights"].tile(e_shape, BF16, tag="e_grouped", align_bytes=64)
-                nc.vector.tensor_copy(
-                    out=e_grouped[:], in_=e_turned[:].rearrange("p (g t) i -> p g i t", t=PACK)
-                )
-                e_codes = pools["weights"].tile([P, KEY_PASSES, P], U32, tag="e_codes", align_bytes=64)
-                e_scales = pools["weights"].tile([P, KEY_PASSES, P], U8, tag="e_scales", align_bytes=64)
-                nc.vector.quantize_mx(
-                    out=e_codes[:].rearrange("p g i -> p (g i)").bitcast(FP8X4),
-                    scales=e_scales[:].rearrange("p g i -> p (g i)"),
-                    in_=e_grouped[:].rearrange("p g i t -> p (g i t)"),
-                )
+        def operands_stage(b):
+            names = ("k", "q", "x", "wv") if b == 0 else ("k", "q", "x")
+            todo = []
+            for name in names:
+                tokens = D if name == "wv" else N
+                new_operand(name, b, tokens)
+                todo.extend([(name, pair) for pair in range(tokens // (2 * P))])
+            turn_input_bank(todo[0][0], b, todo[0][1])
+            for i in range(len(todo)):
+                name, pair = todo[i]
+                if i + 1 < len(todo):
+                    turn_input_bank(todo[i + 1][0], b, todo[i + 1][1])
+                regroup_words(nc, operand[(name, b)][0], banks[(name, b, pair)], pair)
+                if i >= 1:
+                    quantise_input_bank(todo[i - 1][0], b, todo[i - 1][1])
+            quantise_input_bank(todo[-1][0], b, todo[-1][1])
+            spread_key_sums(b)
+            nc.vector.tensor_scalar_mul(new_stat("neg_qq", b)[:], stat[("qq", b)][:], -1.0)
+            nc.vector.tensor_scalar_mul(new_stat("qq_over_d", b)[:], stat[("qq", b)][:], 1.0 / D)
 
-                summed = pools["psum_results"].tile([P, D], F32, tag="summed")
-                for g in range(KEY_PASSES):
-                    nc.tensor.matmul_mx(
-                        out=summed[:],
-                        lhsT=e_codes[:, g, :].bitcast(FP8X4),
-                        lhsT_scale=e_scales[:, g, :],
-                        rhs=v_codes[:, g, :].bitcast(FP8X4),
-                        rhs_scale=v_scales[:, g, :],
-                        start=(g == 0),
-                        stop=(g == KEY_PASSES - 1),
-                    )
-                g, t = divmod(T, PACK)
-                if t == 0:
-                    result = pools["results"].tile([P, PACK, D], F32, tag="result")
-                if T % 2 == 0:
-                    nc.scalar.activation(
-                        out=result[:, t, :],
-                        in_=summed[:],
-                        func=ACT.Copy,
-                        scale=one_over_sum[:, T : T + 1],
-                    )
-                else:
-                    nc.vector.tensor_scalar_mul(
-                        result[:, t, :], summed[:], one_over_sum[:, T : T + 1]
-                    )
-                if t == PACK - 1:
-                    nc.sync.dma_start(out=out_tiles[:, g], in_=result[:])
-
-        ready = prepare(0)
-        for b in range(B):
-            rows, neg_row_max = distances(ready)
-            following = prepare(b + 1) if b + 1 < B else None
-            attend(b, ready, rows, neg_row_max)
-            ready = following
+        start_batch(0)
+        wv_raw = raw_pool.tile([P, D // P, D], BF16, tag="wv_raw", bufs=1)
+        nc.sync.dma_start(out=wv_raw[:], in_=Wv.rearrange("(t p) f -> p t f", p=P))
+        raw[("wv", 0)] = wv_raw
+        start_batch(1)
+        for r in range(-2, B):
+            if r >= -1 and valid(r + 3):
+                start_batch(r + 3)
+            weights_stage(r, r + 2)
+            if valid(r + 1):
+                score_passes(r + 1, 0)
+            if valid(r):
+                weights_stage_end(r)
+            distances_stage(r + 1, r + 2)
+            if valid(r + 2):
+                operands_stage(r + 2)
+            if valid(r + 1):
+                quantise_values(r + 1)

@@ -68,17 +68,17 @@ def tile_attention_pa_t_kernel(tc, q, k, x, Wv, out):
     with ExitStack() as ctx:
         const_pool = ctx.enter_context(tc.tile_pool(name="const", bufs=1))
         raw_pool = ctx.enter_context(tc.tile_pool(name="raw", bufs=2))
-        operand_pool = ctx.enter_context(tc.tile_pool(name="operands", bufs=1))
+        grouped_pool = ctx.enter_context(tc.tile_pool(name="grouped", bufs=2))
+        operand_pool = ctx.enter_context(tc.tile_pool(name="operands", bufs=2))
         scratch_pool = ctx.enter_context(tc.tile_pool(name="scratch", bufs=2))
         stats_pool = ctx.enter_context(tc.tile_pool(name="stats", bufs=2))
-        score_pool = ctx.enter_context(tc.tile_pool(name="scores", bufs=TILES))
+        score_pool = ctx.enter_context(tc.tile_pool(name="scores", bufs=TILES + TILES // 2))
         e_pool = ctx.enter_context(tc.tile_pool(name="e", bufs=TILES))
         weight_pool = ctx.enter_context(tc.tile_pool(name="weights", bufs=3))
         result_pool = ctx.enter_context(tc.tile_pool(name="results", bufs=2))
         psum_staging = ctx.enter_context(tc.psum_pool(name="psum_staging", bufs=2))
         psum_sums = ctx.enter_context(tc.psum_pool(name="psum_sums", bufs=4))
         psum_turned = ctx.enter_context(tc.psum_pool(name="psum_turned", bufs=2))
-        ctx.enter_context(tc.manual_schedule())
 
         ident_words = const_pool.tile([P, P], F32)
         masks.make_identity(nc, ident_words[:])
@@ -101,7 +101,7 @@ def tile_attention_pa_t_kernel(tc, q, k, x, Wv, out):
                 raw[(name, b)] = rows_in
 
         def new_operand(name, b, columns):
-            grouped = operand_pool.tile([P, columns * PACK], BF16, tag=name + "_grouped", align_bytes=64)
+            grouped = grouped_pool.tile([P, columns * PACK], BF16, tag="grouped", align_bytes=64)
             codes = operand_pool.tile([P, columns], U32, tag=name + "_codes", align_bytes=64)
             scales = operand_pool.tile([P, columns], U8, tag=name + "_scales", align_bytes=64)
             operand[(name, b)] = (grouped, codes, scales)
@@ -229,9 +229,6 @@ def tile_attention_pa_t_kernel(tc, q, k, x, Wv, out):
                 in_=banks[("e_turned", b, T)][:].rearrange("p (g t) i -> p g i t", t=PACK),
             )
             weights[("e_grouped", b, T)] = e_grouped
-            nc.vector.reciprocal(
-                stat[("one_over_sum", b)][:, T : T + 1], stat[("row_sum", b)][:, T : T + 1]
-            )
 
         def quantise_weights(b, T):
             e_codes = weight_pool.tile([P, KEY_PASSES * P], U32, tag="e_codes", align_bytes=64)
@@ -305,9 +302,9 @@ def tile_attention_pa_t_kernel(tc, q, k, x, Wv, out):
                 new_stat("kk", ahead)
             if valid(b):
                 new_stat("row_sum", b)
-                new_stat("one_over_sum", b)
                 for T in range(TILES):
                     exponentials(b, T)
+                nc.vector.reciprocal(new_stat("one_over_sum", b)[:], stat[("row_sum", b)][:])
                 turn_weights(b, 0)
             for T in range(TILES):
                 if valid(b):

@@ -20,13 +20,15 @@ KEY_PASSES = N // K_PASS
 BANK = 512
 HALVES = N // BANK
 
+RUN = {"k": 2, "q": 4, "x": 4}
+
 FLOPS = 2 * B * N * D * D + 2 * 2 * B * N * N * D
 
 
-def load_tokens(nc, raw, rows):
+def load_tokens(nc, raw, rows, run):
     nc.sync.dma_start(
-        out=raw[:].rearrange("p (g t) d -> p g t d", t=PACK),
-        in_=rows.rearrange("(g p t) d -> p g t d", p=P, t=PACK),
+        out=raw[:].rearrange("p (g t) d -> p g t d", t=run),
+        in_=rows.rearrange("(g p t) d -> p g t d", p=P, t=run),
     )
 
 
@@ -39,12 +41,18 @@ def turn_words(nc, turned, raw, pair, ident_words):
             )
 
 
-def regroup_words(nc, grouped, turned, pair):
-    grouped_words = grouped[:].bitcast(F32).rearrange("p (c u) -> p c u", u=2)
-    nc.vector.tensor_copy(
-        out=grouped_words[:, pair * 2 * P : (pair + 1) * 2 * P, :],
-        in_=turned[:].rearrange("p u c -> p c u"),
-    )
+def regroup_words(copy, grouped, turned, pair, alternate_tiles):
+    words = grouped[:].bitcast(F32)[:, pair * 4 * P : (pair + 1) * 4 * P]
+    if alternate_tiles:
+        copy(
+            out=words.rearrange("p (c a u) -> p c a u", a=2, u=2),
+            in_=turned[:].rearrange("p u (a c) -> p c a u", a=2),
+        )
+    else:
+        copy(
+            out=words.rearrange("p (c u) -> p c u", u=2),
+            in_=turned[:].rearrange("p u c -> p c u"),
+        )
 
 
 def quantise_columns(nc, codes, scales, grouped, first, count):
@@ -55,10 +63,35 @@ def quantise_columns(nc, codes, scales, grouped, first, count):
     )
 
 
+def token_products(nc, products, grouped, T):
+    values = grouped[:, T * P * PACK : (T + 1) * P * PACK]
+    for t in range(PACK):
+        nc.tensor.matmul(
+            products,
+            lhsT=values[:, t :: PACK],
+            rhs=values[:, t :: PACK],
+            start=(t == 0),
+            stop=(t == PACK - 1),
+        )
+
+
 def square_sum(nc, scratch_pool, sums, raw, T):
     squares = scratch_pool.tile([P, D], BF16, tag="squares")
     nc.scalar.activation(
         out=squares[:], in_=raw[:, T, :], func=ACT.Square, accum_out=sums[:, T : T + 1]
+    )
+
+
+def diagonal_sum(nc, scratch_pool, sums, products, ident_words, T):
+    diagonal = scratch_pool.tile([P, P], F32, tag="diagonal")
+    nc.vector.scalar_tensor_tensor(
+        out=diagonal[:],
+        in0=products,
+        scalar=1.0,
+        in1=ident_words[:],
+        op0=ALU.mult,
+        op1=ALU.mult,
+        accum_out=sums[:, T : T + 1],
     )
 
 
@@ -68,12 +101,12 @@ def tile_attention_pa_t_kernel(tc, q, k, x, Wv, out):
     with ExitStack() as ctx:
         const_pool = ctx.enter_context(tc.tile_pool(name="const", bufs=1))
         raw_pool = ctx.enter_context(tc.tile_pool(name="raw", bufs=2))
-        grouped_pool = ctx.enter_context(tc.tile_pool(name="grouped", bufs=2))
+        grouped_pool = ctx.enter_context(tc.tile_pool(name="grouped", bufs=3))
         operand_pool = ctx.enter_context(tc.tile_pool(name="operands", bufs=2))
         scratch_pool = ctx.enter_context(tc.tile_pool(name="scratch", bufs=2))
         stats_pool = ctx.enter_context(tc.tile_pool(name="stats", bufs=2))
-        score_pool = ctx.enter_context(tc.tile_pool(name="scores", bufs=TILES + TILES // 2))
-        e_pool = ctx.enter_context(tc.tile_pool(name="e", bufs=TILES))
+        score_pool = ctx.enter_context(tc.tile_pool(name="scores", bufs=2 * TILES))
+        e_pool = ctx.enter_context(tc.tile_pool(name="e", bufs=4))
         weight_pool = ctx.enter_context(tc.tile_pool(name="weights", bufs=3))
         result_pool = ctx.enter_context(tc.tile_pool(name="results", bufs=2))
         psum_staging = ctx.enter_context(tc.psum_pool(name="psum_staging", bufs=2))
@@ -82,8 +115,6 @@ def tile_attention_pa_t_kernel(tc, q, k, x, Wv, out):
 
         ident_words = const_pool.tile([P, P], F32)
         masks.make_identity(nc, ident_words[:])
-        ident_bf16 = const_pool.tile([P, P], BF16)
-        masks.make_identity(nc, ident_bf16[:])
 
         raw = {}
         operand = {}
@@ -97,7 +128,7 @@ def tile_attention_pa_t_kernel(tc, q, k, x, Wv, out):
         def start_batch(b):
             for name in ("k", "q", "x"):
                 rows_in = raw_pool.tile([P, TILES, D], BF16, tag=name + "_raw")
-                load_tokens(nc, rows_in, inputs[name][b])
+                load_tokens(nc, rows_in, inputs[name][b], RUN[name])
                 raw[(name, b)] = rows_in
 
         def new_operand(name, b, columns):
@@ -110,6 +141,20 @@ def tile_attention_pa_t_kernel(tc, q, k, x, Wv, out):
             column_per_tile = stats_pool.tile([P, TILES], F32, tag=name)
             stat[(name, b)] = column_per_tile
             return column_per_tile
+
+
+        def regroup_on_vector(b, i):
+            if b == 0:
+                return i % 2 == 0
+            if b == 1:
+                return False
+            return not (b == B - 1 and i >= 8)
+
+        def group_on_vector(b, T):
+            return b >= B - 2 or T % 4 == 3
+
+        def divide_on_vector(b, T):
+            return b >= B - 2 and T % 4 != 3
 
 
         def score_passes(b, T):
@@ -175,9 +220,9 @@ def tile_attention_pa_t_kernel(tc, q, k, x, Wv, out):
             wv_codes, wv_scales = operand[("wv", 0)][1:]
             g, c = divmod(C, D // P)
             if C % 2 == 0:
-                values = psum_staging.tile([P, PACK, P], F32, tag="staging")
-            else:
                 values = psum_turned.tile([P, PACK, P], F32, tag="e_turned")
+            else:
+                values = psum_sums.tile([P, PACK, P], F32, tag="sums")
             for t in range(PACK):
                 T = g * PACK + t
                 nc.tensor.matmul_mx(
@@ -215,18 +260,29 @@ def tile_attention_pa_t_kernel(tc, q, k, x, Wv, out):
             )
             weights[("e", b, T)] = e
 
+        def invert_sums(b, T):
+            nc.vector.reciprocal(
+                stat[("one_over_sum", b)][:, T : T + 2], stat[("row_sum", b)][:, T : T + 2]
+            )
+
         def turn_weights(b, T):
-            e = weights[("e", b, T)]
-            e_turned = psum_turned.tile([P, TILES, P], BF16, tag="e_turned")
-            for J in range(TILES):
-                nc.tensor.transpose(e_turned[:, J, :], e[:, J * P : (J + 1) * P], ident_bf16[:])
+            words = weights[("e", b, T)][:].bitcast(F32)
+            e_turned = psum_turned.tile([P, KEY_PASSES, 2, P], F32, tag="e_turned")
+            for g in range(KEY_PASSES):
+                for u in range(2):
+                    nc.tensor.transpose(
+                        e_turned[:, g, u, :],
+                        words[:, g * 2 * P + u : (g + 1) * 2 * P : 2],
+                        ident_words[:],
+                    )
             banks[("e_turned", b, T)] = e_turned
 
         def group_weights(b, T):
             e_grouped = weight_pool.tile([P, KEY_PASSES * P * PACK], BF16, tag="e_grouped", align_bytes=64)
-            nc.vector.tensor_copy(
-                out=e_grouped[:].rearrange("p (g i t) -> p g i t", g=KEY_PASSES, t=PACK),
-                in_=banks[("e_turned", b, T)][:].rearrange("p (g t) i -> p g i t", t=PACK),
+            copy = nc.vector.tensor_copy if group_on_vector(b, T) else nc.scalar.copy
+            copy(
+                out=e_grouped[:].bitcast(F32).rearrange("p (g i u) -> p g i u", g=KEY_PASSES, u=2),
+                in_=banks[("e_turned", b, T)][:].rearrange("p g u i -> p g i u"),
             )
             weights[("e_grouped", b, T)] = e_grouped
 
@@ -239,7 +295,7 @@ def tile_attention_pa_t_kernel(tc, q, k, x, Wv, out):
         def weighted_sum(b, T):
             e_codes, e_scales = weights[("e_codes", b, T)]
             v_codes, v_scales = operand[("v", b)][1:]
-            summed = psum_sums.tile([P, D], F32, tag="sums")
+            summed = psum_staging.tile([P, D], F32, tag="staging")
             for g in range(KEY_PASSES):
                 nc.tensor.matmul_mx(
                     out=summed[:],
@@ -257,12 +313,18 @@ def tile_attention_pa_t_kernel(tc, q, k, x, Wv, out):
             if t == 0:
                 four_tiles = result_pool.tile([P, PACK, D], F32, tag="result")
                 results[(b, g)] = four_tiles
-            nc.scalar.activation(
-                out=results[(b, g)][:, t, :],
-                in_=banks[("summed", b, T)][:],
-                func=ACT.Copy,
-                scale=stat[("one_over_sum", b)][:, T : T + 1],
-            )
+            one_over_sum = stat[("one_over_sum", b)][:, T : T + 1]
+            if divide_on_vector(b, T):
+                nc.vector.tensor_scalar_mul(
+                    results[(b, g)][:, t, :], banks[("summed", b, T)][:], one_over_sum
+                )
+            else:
+                nc.scalar.activation(
+                    out=results[(b, g)][:, t, :],
+                    in_=banks[("summed", b, T)][:],
+                    func=ACT.Copy,
+                    scale=one_over_sum,
+                )
             if t == PACK - 1:
                 out_tiles = out[b].rearrange("(g p t) d -> p g t d", p=P, t=PACK)
                 nc.sync.dma_start(out=out_tiles[:, g], in_=results[(b, g)][:])
@@ -275,6 +337,19 @@ def tile_attention_pa_t_kernel(tc, q, k, x, Wv, out):
         def quantise_input_bank(name, b, pair):
             grouped, codes, scales = operand[(name, b)]
             quantise_columns(nc, codes, scales, grouped, pair * 2 * P, 2 * P)
+
+        def multiply_keys(b, pair):
+            products = psum_sums.tile([P, 2, P], F32, tag="sums")
+            for a in range(2):
+                token_products(nc, products[:, a, :], operand[("k", b)][0], 2 * pair + a)
+            banks[("products", b, pair)] = products
+
+        def sum_key_squares(b, pair):
+            products = banks[("products", b, pair)]
+            for a in range(2):
+                diagonal_sum(
+                    nc, scratch_pool, stat[("kk", b)], products[:, a, :], ident_words, 2 * pair + a
+                )
 
         def spread_key_sums(b):
             spread_rows = operand_pool.tile([P, N], F32, tag="kk_rows")
@@ -297,95 +372,137 @@ def tile_attention_pa_t_kernel(tc, q, k, x, Wv, out):
         def valid(b):
             return 0 <= b < B
 
-        def weights_stage(b, ahead):
-            if valid(ahead):
-                new_stat("kk", ahead)
-            if valid(b):
-                new_stat("row_sum", b)
-                for T in range(TILES):
-                    exponentials(b, T)
-                nc.vector.reciprocal(new_stat("one_over_sum", b)[:], stat[("row_sum", b)][:])
-                turn_weights(b, 0)
-            for T in range(TILES):
-                if valid(b):
-                    if T + 1 < TILES:
-                        turn_weights(b, T + 1)
-                    group_weights(b, T)
-                    if T >= 1:
-                        quantise_weights(b, T - 1)
-                        weighted_sum(b, T - 1)
-                    if T >= 2:
-                        divide_and_store(b, T - 2)
-                if valid(ahead):
-                    square_sum(nc, scratch_pool, stat[("kk", ahead)], raw[("k", ahead)], T)
-
-        def weights_stage_end(b):
-            quantise_weights(b, TILES - 1)
-            weighted_sum(b, TILES - 1)
-            divide_and_store(b, TILES - 2)
-            divide_and_store(b, TILES - 1)
-
-        def distances_stage(b, ahead):
-            if valid(ahead):
-                new_stat("qq", ahead)
-            if valid(b):
-                new_operand("v", b, KEY_PASSES * D)
-                new_stat("peak", b)
-            for T in range(TILES):
-                if valid(b):
-                    if T + 1 < TILES:
-                        score_passes(b, T + 1)
-                    value_passes(b, T)
-                    keys_minus_products(b, T)
-                    if T >= 1:
-                        clamp_and_peak(b, T - 1)
-                if valid(ahead):
-                    square_sum(nc, scratch_pool, stat[("qq", ahead)], raw[("q", ahead)], T)
-                if valid(b):
-                    round_values(b, T)
-                    if T >= 2:
-                        square_root(b, T - 2)
-            if valid(b):
-                clamp_and_peak(b, TILES - 1)
-                square_root(b, TILES - 2)
-                square_root(b, TILES - 1)
-                row_maxima(b)
-
-        def operands_stage(b):
+        def input_banks(b):
             names = ("k", "q", "x", "wv") if b == 0 else ("k", "q", "x")
-            todo = []
+            banks_in_order = []
             for name in names:
                 tokens = D if name == "wv" else N
-                new_operand(name, b, tokens)
-                todo.extend([(name, pair) for pair in range(tokens // (2 * P))])
-            turn_input_bank(todo[0][0], b, todo[0][1])
-            for i in range(len(todo)):
+                banks_in_order.extend([(name, pair) for pair in range(tokens // (2 * P))])
+            return banks_in_order
+
+        def operand_step(b, i):
+            todo = input_banks(b)
+            if i == 0:
+                new_stat("kk", b)
+                new_stat("qq", b)
+            if i + 1 < len(todo):
+                name, pair = todo[i + 1]
+                if pair == 0:
+                    new_operand(name, b, D if name == "wv" else N)
+                turn_input_bank(name, b, pair)
+            if 0 <= i < len(todo):
                 name, pair = todo[i]
-                if i + 1 < len(todo):
-                    turn_input_bank(todo[i + 1][0], b, todo[i + 1][1])
-                regroup_words(nc, operand[(name, b)][0], banks[(name, b, pair)], pair)
-                if i >= 1:
-                    quantise_input_bank(todo[i - 1][0], b, todo[i - 1][1])
-            quantise_input_bank(todo[-1][0], b, todo[-1][1])
-            spread_key_sums(b)
-            nc.vector.tensor_scalar_mul(new_stat("neg_qq", b)[:], stat[("qq", b)][:], -1.0)
-            nc.vector.tensor_scalar_mul(new_stat("qq_over_d", b)[:], stat[("qq", b)][:], 1.0 / D)
+                copy = nc.vector.tensor_copy if regroup_on_vector(b, i) else nc.scalar.copy
+                regroup_words(copy, operand[(name, b)][0], banks[(name, b, pair)], pair, name == "k")
+                if name == "q":
+                    for a in range(2):
+                        square_sum(nc, scratch_pool, stat[("qq", b)], raw[("q", b)], 2 * pair + a)
+            if 0 <= i - 1 < len(todo):
+                name, pair = todo[i - 1]
+                quantise_input_bank(name, b, pair)
+                if name == "k":
+                    multiply_keys(b, pair)
+                if (name, pair) == ("x", 0):
+                    nc.vector.tensor_scalar_mul(new_stat("neg_qq", b)[:], stat[("qq", b)][:], -1.0)
+                    nc.vector.tensor_scalar_mul(new_stat("qq_over_d", b)[:], stat[("qq", b)][:], 1.0 / D)
+
+            if 0 <= i - 2 < len(todo):
+                name, pair = todo[i - 2]
+                if name == "k":
+                    sum_key_squares(b, pair)
+                if (name, pair) == ("q", 0):
+                    spread_key_sums(b)
+
+        def first_operand_bank(b):
+            new_operand("k", b, N)
+            turn_input_bank("k", b, 0)
+
+        OPERAND_STEPS = 13
+
+        def score_step(b, T):
+            if T == 0:
+                new_stat("peak", b)
+            if T + 1 < TILES:
+                score_passes(b, T + 1)
+            if T < TILES:
+                keys_minus_products(b, T)
+            if 0 <= T - 1 < TILES:
+                clamp_and_peak(b, T - 1)
+
+        def weight_step(b, T):
+            if T == 0:
+                new_stat("row_sum", b)
+                new_stat("one_over_sum", b)
+            if T < TILES:
+                exponentials(b, T)
+            if T == 2:
+                quantise_values(b)
+            if 0 <= T - 1 < TILES:
+                turn_weights(b, T - 1)
+            if 0 <= T - 2 < TILES:
+                group_weights(b, T - 2)
+            if 0 <= T - 3 < TILES:
+                quantise_weights(b, T - 3)
+                weighted_sum(b, T - 3)
+            if 0 <= T - 2 < TILES and T % 2 == 1:
+                invert_sums(b, T - 3)
+            if 0 <= T - 5 < TILES:
+                divide_and_store(b, T - 5)
+
+        WEIGHT_STEPS = TILES + 5
+
+        def root_step(b, T):
+            if T == 0:
+                new_operand("v", b, KEY_PASSES * D)
+            if T < TILES:
+                value_passes(b, T)
+                square_root(b, T)
+            if 0 <= T - 1 < TILES:
+                round_values(b, T - 1)
+            if T == TILES:
+                row_maxima(b)
+
+        ROOT_STEPS = TILES + 1
 
         start_batch(0)
         wv_raw = raw_pool.tile([P, D // P, D], BF16, tag="wv_raw", bufs=1)
         nc.sync.dma_start(out=wv_raw[:], in_=Wv.rearrange("(t p) f -> p t f", p=P))
         raw[("wv", 0)] = wv_raw
         start_batch(1)
-        for r in range(-2, B):
-            if r >= -1 and valid(r + 3):
-                start_batch(r + 3)
-            weights_stage(r, r + 2)
-            if valid(r + 1):
-                score_passes(r + 1, 0)
-            if valid(r):
-                weights_stage_end(r)
-            distances_stage(r + 1, r + 2)
-            if valid(r + 2):
-                operands_stage(r + 2)
-            if valid(r + 1):
-                quantise_values(r + 1)
+        first_operand_bank(0)
+        for i in range(len(input_banks(0)) + 1):
+            operand_step(0, i)
+        score_passes(0, 0)
+        first_operand_bank(1)
+        start_batch(2)
+        for T in range(OPERAND_STEPS):
+            score_step(0, T)
+            operand_step(1, T)
+            if T >= 3:
+                root_step(0, T - 3)
+        for T in range(OPERAND_STEPS - 3, ROOT_STEPS):
+            root_step(0, T)
+        for b in range(2):
+            if valid(b + 3):
+                start_batch(b + 3)
+            score_passes(b + 1, 0)
+            for T in range(TILES):
+                weight_step(b, T)
+                score_step(b + 1, T)
+            first_operand_bank(b + 2)
+            for T in range(OPERAND_STEPS):
+                weight_step(b, TILES + T)
+                score_step(b + 1, TILES + T)
+                root_step(b + 1, T)
+                operand_step(b + 2, T)
+        score_passes(B - 1, 0)
+        for T in range(TILES + ROOT_STEPS):
+            score_step(B - 1, T)
+            if T >= 2:
+                root_step(B - 1, T - 2)
+        for T in range(WEIGHT_STEPS):
+            weight_step(B - 2, T)
+            if T >= TILES:
+                weight_step(B - 1, T - TILES)
+        for T in range(WEIGHT_STEPS - TILES, WEIGHT_STEPS):
+            weight_step(B - 1, T)

@@ -20,7 +20,7 @@ KEY_PASSES = N // K_PASS
 BANK = 512
 HALVES = N // BANK
 
-RUN = {"k": 2, "q": 4, "x": 4}
+RUN = {"k": 2, "q": 4, "x": 2}
 
 FLOPS = 2 * B * N * D * D + 2 * 2 * B * N * N * D
 
@@ -272,7 +272,7 @@ def tile_attention_pa_t_kernel(tc, q, k, x, Wv, out):
                 for u in range(2):
                     nc.tensor.transpose(
                         e_turned[:, g, u, :],
-                        words[:, g * 2 * P + u : (g + 1) * 2 * P : 2],
+                        words[:, (2 * g + u) * P : (2 * g + u + 1) * P],
                         ident_words[:],
                     )
             banks[("e_turned", b, T)] = e_turned

@@ -25,11 +25,14 @@ RUN = {"k": 2, "q": 4, "x": 2}
 FLOPS = 2 * B * N * D * D + 2 * 2 * B * N * N * D
 
 
-def load_tokens(nc, raw, rows, run):
-    nc.sync.dma_start(
-        out=raw[:].rearrange("p (g t) d -> p g t d", t=run),
-        in_=rows.rearrange("(g p t) d -> p g t d", p=P, t=run),
-    )
+def load_tokens(nc, raw, rows, run, in_parts):
+    tiles = raw[:].rearrange("p (g t) d -> p g t d", t=run)
+    rows = rows.rearrange("(g p t) d -> p g t d", p=P, t=run)
+    if in_parts:
+        for g in range(TILES // run):
+            nc.sync.dma_start(out=tiles[:, g], in_=rows[:, g])
+    else:
+        nc.sync.dma_start(out=tiles, in_=rows)
 
 
 def turn_words(nc, turned, raw, pair, ident_words):
@@ -109,8 +112,8 @@ def tile_attention_pa_t_kernel(tc, q, k, x, Wv, out):
         e_pool = ctx.enter_context(tc.tile_pool(name="e", bufs=4))
         weight_pool = ctx.enter_context(tc.tile_pool(name="weights", bufs=3))
         result_pool = ctx.enter_context(tc.tile_pool(name="results", bufs=2))
-        psum_staging = ctx.enter_context(tc.psum_pool(name="psum_staging", bufs=2))
-        psum_sums = ctx.enter_context(tc.psum_pool(name="psum_sums", bufs=4))
+        psum_staging = ctx.enter_context(tc.psum_pool(name="psum_staging", bufs=3))
+        psum_sums = ctx.enter_context(tc.psum_pool(name="psum_sums", bufs=3))
         psum_turned = ctx.enter_context(tc.psum_pool(name="psum_turned", bufs=2))
 
         ident_words = const_pool.tile([P, P], F32)
@@ -126,9 +129,12 @@ def tile_attention_pa_t_kernel(tc, q, k, x, Wv, out):
         results = {}
 
         def start_batch(b):
+            if b % 2 == 0:
+                for name in ("kk", "qq", "neg_qq", "qq_over_d", "peak", "row_sum", "one_over_sum"):
+                    new_stat(name, b)
             for name in ("k", "q", "x"):
                 rows_in = raw_pool.tile([P, TILES, D], BF16, tag=name + "_raw")
-                load_tokens(nc, rows_in, inputs[name][b], RUN[name])
+                load_tokens(nc, rows_in, inputs[name][b], RUN[name], b == 0)
                 raw[(name, b)] = rows_in
 
         def new_operand(name, b, columns):
@@ -138,9 +144,17 @@ def tile_attention_pa_t_kernel(tc, q, k, x, Wv, out):
             operand[(name, b)] = (grouped, codes, scales)
 
         def new_stat(name, b):
-            column_per_tile = stats_pool.tile([P, TILES], F32, tag=name)
-            stat[(name, b)] = column_per_tile
+            column_per_tile = stats_pool.tile([P, 2 * TILES], F32, tag=name)
+            stat[(name, b // 2)] = column_per_tile
             return column_per_tile
+
+        def column(name, b, T):
+            place = b % 2 * TILES + T
+            return stat[(name, b // 2)][:, place : place + 1]
+
+        def columns(name, b):
+            place = b % 2 * TILES
+            return stat[(name, b // 2)][:, place : place + TILES]
 
 
         def regroup_on_vector(b, i):
@@ -148,10 +162,10 @@ def tile_attention_pa_t_kernel(tc, q, k, x, Wv, out):
                 return i % 2 == 0
             if b == 1:
                 return False
-            return not (b == B - 1 and i >= 8)
+            return True
 
         def group_on_vector(b, T):
-            return b >= B - 2 or T % 4 == 3
+            return b >= B - 2
 
         def divide_on_vector(b, T):
             return b >= B - 2 and T % 4 != 3
@@ -190,11 +204,11 @@ def tile_attention_pa_t_kernel(tc, q, k, x, Wv, out):
             nc.vector.tensor_scalar(
                 out=rows[(b, T)][:],
                 in0=rows[(b, T)][:],
-                scalar1=stat[("neg_qq", b)][:, T : T + 1],
+                scalar1=column("neg_qq", b, T),
                 scalar2=None,
                 op0=ALU.max,
                 op1=ALU.max,
-                accum_out=stat[("peak", b)][:, T : T + 1],
+                accum_out=column("peak", b, T),
             )
 
         def square_root(b, T):
@@ -202,14 +216,14 @@ def tile_attention_pa_t_kernel(tc, q, k, x, Wv, out):
                 out=rows[(b, T)][:],
                 in_=rows[(b, T)][:],
                 func=ACT.Sqrt,
-                bias=stat[("qq_over_d", b)][:, T : T + 1],
+                bias=column("qq_over_d", b, T),
                 scale=1.0 / D,
             )
 
         def row_maxima(b):
             largest_d2 = new_stat("largest_d2", b)
             nc.vector.tensor_tensor(
-                out=largest_d2[:], in0=stat[("peak", b)][:], in1=stat[("qq", b)][:], op=ALU.add
+                out=largest_d2[:], in0=stat[("peak", b // 2)][:], in1=stat[("qq", b // 2)][:], op=ALU.add
             )
             row_max = new_stat("row_max", b)
             nc.scalar.activation(out=row_max[:], in_=largest_d2[:], func=ACT.Sqrt, scale=1.0 / D)
@@ -219,10 +233,7 @@ def tile_attention_pa_t_kernel(tc, q, k, x, Wv, out):
             x_codes, x_scales = operand[("x", b)][1:]
             wv_codes, wv_scales = operand[("wv", 0)][1:]
             g, c = divmod(C, D // P)
-            if C % 2 == 0:
-                values = psum_turned.tile([P, PACK, P], F32, tag="e_turned")
-            else:
-                values = psum_sums.tile([P, PACK, P], F32, tag="sums")
+            values = psum_turned.tile([P, PACK, P], F32, tag="e_turned")
             for t in range(PACK):
                 T = g * PACK + t
                 nc.tensor.matmul_mx(
@@ -254,15 +265,15 @@ def tile_attention_pa_t_kernel(tc, q, k, x, Wv, out):
                 out=e[:],
                 in_=rows[(b, T)][:],
                 func=ACT.Exp,
-                bias=stat[("neg_row_max", b)][:, T : T + 1],
+                bias=column("neg_row_max", b, T),
                 scale=1.0,
-                accum_out=stat[("row_sum", b)][:, T : T + 1],
+                accum_out=column("row_sum", b, T),
             )
             weights[("e", b, T)] = e
 
         def invert_sums(b, T):
             nc.vector.reciprocal(
-                stat[("one_over_sum", b)][:, T : T + 2], stat[("row_sum", b)][:, T : T + 2]
+                columns("one_over_sum", b)[:, T : T + 2], columns("row_sum", b)[:, T : T + 2]
             )
 
         def turn_weights(b, T):
@@ -313,7 +324,7 @@ def tile_attention_pa_t_kernel(tc, q, k, x, Wv, out):
             if t == 0:
                 four_tiles = result_pool.tile([P, PACK, D], F32, tag="result")
                 results[(b, g)] = four_tiles
-            one_over_sum = stat[("one_over_sum", b)][:, T : T + 1]
+            one_over_sum = column("one_over_sum", b, T)
             if divide_on_vector(b, T):
                 nc.vector.tensor_scalar_mul(
                     results[(b, g)][:, t, :], banks[("summed", b, T)][:], one_over_sum
@@ -325,8 +336,10 @@ def tile_attention_pa_t_kernel(tc, q, k, x, Wv, out):
                     func=ACT.Copy,
                     scale=one_over_sum,
                 )
-            if t == PACK - 1:
-                out_tiles = out[b].rearrange("(g p t) d -> p g t d", p=P, t=PACK)
+            out_tiles = out[b].rearrange("(g p t) d -> p g t d", p=P, t=PACK)
+            if (b, g) == (B - 1, TILES // PACK - 1):
+                nc.sync.dma_start(out=out_tiles[:, g, t], in_=results[(b, g)][:, t])
+            elif t == PACK - 1:
                 nc.sync.dma_start(out=out_tiles[:, g], in_=results[(b, g)][:])
 
         def turn_input_bank(name, b, pair):
@@ -348,7 +361,7 @@ def tile_attention_pa_t_kernel(tc, q, k, x, Wv, out):
             products = banks[("products", b, pair)]
             for a in range(2):
                 diagonal_sum(
-                    nc, scratch_pool, stat[("kk", b)], products[:, a, :], ident_words, 2 * pair + a
+                    nc, scratch_pool, columns("kk", b), products[:, a, :], ident_words, 2 * pair + a
                 )
 
         def spread_key_sums(b):
@@ -359,7 +372,7 @@ def tile_attention_pa_t_kernel(tc, q, k, x, Wv, out):
                     T = h * PACK + t
                     nc.tensor.transpose(
                         spread[:, t, :],
-                        stat[("kk", b)][:, T : T + 1].to_broadcast([P, P]),
+                        column("kk", b, T).to_broadcast([P, P]),
                         ident_words[:],
                     )
                 nc.vector.tensor_copy(
@@ -368,9 +381,6 @@ def tile_attention_pa_t_kernel(tc, q, k, x, Wv, out):
                 )
             kk_rows[b] = spread_rows
 
-
-        def valid(b):
-            return 0 <= b < B
 
         def input_banks(b):
             names = ("k", "q", "x", "wv") if b == 0 else ("k", "q", "x")
@@ -382,9 +392,6 @@ def tile_attention_pa_t_kernel(tc, q, k, x, Wv, out):
 
         def operand_step(b, i):
             todo = input_banks(b)
-            if i == 0:
-                new_stat("kk", b)
-                new_stat("qq", b)
             if i + 1 < len(todo):
                 name, pair = todo[i + 1]
                 if pair == 0:
@@ -394,18 +401,11 @@ def tile_attention_pa_t_kernel(tc, q, k, x, Wv, out):
                 name, pair = todo[i]
                 copy = nc.vector.tensor_copy if regroup_on_vector(b, i) else nc.scalar.copy
                 regroup_words(copy, operand[(name, b)][0], banks[(name, b, pair)], pair, name == "k")
-                if name == "q":
-                    for a in range(2):
-                        square_sum(nc, scratch_pool, stat[("qq", b)], raw[("q", b)], 2 * pair + a)
             if 0 <= i - 1 < len(todo):
                 name, pair = todo[i - 1]
                 quantise_input_bank(name, b, pair)
                 if name == "k":
                     multiply_keys(b, pair)
-                if (name, pair) == ("x", 0):
-                    nc.vector.tensor_scalar_mul(new_stat("neg_qq", b)[:], stat[("qq", b)][:], -1.0)
-                    nc.vector.tensor_scalar_mul(new_stat("qq_over_d", b)[:], stat[("qq", b)][:], 1.0 / D)
-
             if 0 <= i - 2 < len(todo):
                 name, pair = todo[i - 2]
                 if name == "k":
@@ -413,30 +413,41 @@ def tile_attention_pa_t_kernel(tc, q, k, x, Wv, out):
                 if (name, pair) == ("q", 0):
                     spread_key_sums(b)
 
-        def first_operand_bank(b):
-            new_operand("k", b, N)
-            turn_input_bank("k", b, 0)
+        def operand_steps(b):
+            return range(-1, len(input_banks(b)) + 1)
 
-        OPERAND_STEPS = 13
+        def query_square_step(b, T):
+            square_sum(nc, scratch_pool, columns("qq", b), raw[("q", b)], T)
+            if T == TILES - 1:
+                nc.vector.tensor_scalar_mul(columns("neg_qq", b), columns("qq", b), -1.0)
+                nc.vector.tensor_scalar_mul(columns("qq_over_d", b), columns("qq", b), 1.0 / D)
 
         def score_step(b, T):
-            if T == 0:
-                new_stat("peak", b)
             if T + 1 < TILES:
                 score_passes(b, T + 1)
-            if T < TILES:
+            if 0 <= T < TILES:
                 keys_minus_products(b, T)
             if 0 <= T - 1 < TILES:
                 clamp_and_peak(b, T - 1)
 
+        def root_step(b, T):
+            square_root(b, T)
+            if b % 2 == 1 and T == TILES - 1:
+                row_maxima(b)
+
+        def value_step(b, C):
+            if C == 0:
+                new_operand("v", b, KEY_PASSES * D)
+            if C < TILES:
+                value_passes(b, C)
+            if C >= 1:
+                round_values(b, C - 1)
+            if C == TILES:
+                quantise_values(b)
+
         def weight_step(b, T):
-            if T == 0:
-                new_stat("row_sum", b)
-                new_stat("one_over_sum", b)
             if T < TILES:
                 exponentials(b, T)
-            if T == 2:
-                quantise_values(b)
             if 0 <= T - 1 < TILES:
                 turn_weights(b, T - 1)
             if 0 <= T - 2 < TILES:
@@ -444,65 +455,68 @@ def tile_attention_pa_t_kernel(tc, q, k, x, Wv, out):
             if 0 <= T - 3 < TILES:
                 quantise_weights(b, T - 3)
                 weighted_sum(b, T - 3)
-            if 0 <= T - 2 < TILES and T % 2 == 1:
-                invert_sums(b, T - 3)
-            if 0 <= T - 5 < TILES:
-                divide_and_store(b, T - 5)
-
-        WEIGHT_STEPS = TILES + 5
-
-        def root_step(b, T):
-            if T == 0:
-                new_operand("v", b, KEY_PASSES * D)
-            if T < TILES:
-                value_passes(b, T)
-                square_root(b, T)
-            if 0 <= T - 1 < TILES:
-                round_values(b, T - 1)
-            if T == TILES:
-                row_maxima(b)
-
-        ROOT_STEPS = TILES + 1
+                if T % 2 == 0:
+                    invert_sums(b, T - 4)
+            if 0 <= T - 4 < TILES:
+                divide_and_store(b, T - 4)
 
         start_batch(0)
         wv_raw = raw_pool.tile([P, D // P, D], BF16, tag="wv_raw", bufs=1)
         nc.sync.dma_start(out=wv_raw[:], in_=Wv.rearrange("(t p) f -> p t f", p=P))
         raw[("wv", 0)] = wv_raw
         start_batch(1)
-        first_operand_bank(0)
-        for i in range(len(input_banks(0)) + 1):
+        for i in operand_steps(0):
             operand_step(0, i)
-        score_passes(0, 0)
-        first_operand_bank(1)
+            if i >= 1 and i - 1 < TILES:
+                query_square_step(0, i - 1)
         start_batch(2)
-        for T in range(OPERAND_STEPS):
-            score_step(0, T)
-            operand_step(1, T)
-            if T >= 3:
-                root_step(0, T - 3)
-        for T in range(OPERAND_STEPS - 3, ROOT_STEPS):
-            root_step(0, T)
-        for b in range(2):
-            if valid(b + 3):
-                start_batch(b + 3)
-            score_passes(b + 1, 0)
-            for T in range(TILES):
-                weight_step(b, T)
-                score_step(b + 1, T)
-            first_operand_bank(b + 2)
-            for T in range(OPERAND_STEPS):
-                weight_step(b, TILES + T)
-                score_step(b + 1, TILES + T)
-                root_step(b + 1, T)
-                operand_step(b + 2, T)
-        score_passes(B - 1, 0)
-        for T in range(TILES + ROOT_STEPS):
-            score_step(B - 1, T)
-            if T >= 2:
-                root_step(B - 1, T - 2)
-        for T in range(WEIGHT_STEPS):
-            weight_step(B - 2, T)
-            if T >= TILES:
-                weight_step(B - 1, T - TILES)
-        for T in range(WEIGHT_STEPS - TILES, WEIGHT_STEPS):
-            weight_step(B - 1, T)
+        for i in range(13):
+            if i - 1 <= TILES:
+                score_step(0, i - 1)
+            operand_step(1, i - 1)
+            if i < TILES:
+                query_square_step(1, i)
+            if 3 <= i < 3 + TILES:
+                root_step(0, i - 3)
+            if i < TILES + 1:
+                value_step(0, i)
+        operand_step(1, 12)
+        for i in range(13):
+            if i - 1 <= TILES:
+                score_step(1, i - 1)
+            if i < TILES:
+                query_square_step(2, i)
+            if i < TILES + 1:
+                value_step(1, i)
+            if 3 <= i < 3 + TILES:
+                root_step(1, i - 3)
+        start_batch(3)
+        for i in range(2 * TILES + 4):
+            if i < TILES + 4:
+                weight_step(0, i)
+            if i >= TILES:
+                weight_step(1, i - TILES)
+            if i < 7:
+                for n in (2 * i - 1, 2 * i):
+                    operand_step(2, n)
+            elif i - 7 - 1 <= TILES:
+                score_step(2, i - 7 - 1)
+        for i in range(14):
+            operand_step(3, i - 1)
+            if i < TILES:
+                query_square_step(3, i)
+                root_step(2, i)
+            if 4 <= i < 4 + TILES + 1:
+                value_step(2, i - 4)
+        for i in range(13):
+            if i - 1 <= TILES:
+                score_step(3, i - 1)
+            if i < TILES + 1:
+                value_step(3, i)
+            if 3 <= i < 3 + TILES:
+                root_step(3, i - 3)
+        for i in range(2 * TILES + 4):
+            if i < TILES + 4:
+                weight_step(2, i)
+            if i >= TILES:
+                weight_step(3, i - TILES)

@@ -158,11 +158,7 @@ def tile_attention_pa_t_kernel(tc, q, k, x, Wv, out):
 
 
         def regroup_on_vector(b, i):
-            if b == 0:
-                return i % 2 == 0
-            if b == 1:
-                return False
-            return True
+            return b >= 2 or b == 0 and i % 4 == 0
 
         def group_on_vector(b, T):
             return b >= B - 2
@@ -273,7 +269,7 @@ def tile_attention_pa_t_kernel(tc, q, k, x, Wv, out):
 
         def invert_sums(b, T):
             nc.vector.reciprocal(
-                columns("one_over_sum", b)[:, T : T + 2], columns("row_sum", b)[:, T : T + 2]
+                columns("one_over_sum", b)[:, T : T + PACK], columns("row_sum", b)[:, T : T + PACK]
             )
 
         def turn_weights(b, T):
@@ -347,21 +343,21 @@ def tile_attention_pa_t_kernel(tc, q, k, x, Wv, out):
             turn_words(nc, turned, raw[(name, b)], pair, ident_words)
             banks[(name, b, pair)] = turned
 
-        def quantise_input_bank(name, b, pair):
+        def quantise_input_banks(name, b, pair):
             grouped, codes, scales = operand[(name, b)]
-            quantise_columns(nc, codes, scales, grouped, pair * 2 * P, 2 * P)
+            quantise_columns(nc, codes, scales, grouped, (pair - 1) * 2 * P, 4 * P)
 
-        def multiply_keys(b, pair):
+        def multiply_tokens(name, b, pair):
             products = psum_sums.tile([P, 2, P], F32, tag="sums")
             for a in range(2):
-                token_products(nc, products[:, a, :], operand[("k", b)][0], 2 * pair + a)
-            banks[("products", b, pair)] = products
+                token_products(nc, products[:, a, :], operand[(name, b)][0], 2 * pair + a)
+            banks[("products", name, b, pair)] = products
 
-        def sum_key_squares(b, pair):
-            products = banks[("products", b, pair)]
+        def sum_squares(name, b, pair):
+            products = banks[("products", name, b, pair)]
             for a in range(2):
                 diagonal_sum(
-                    nc, scratch_pool, columns("kk", b), products[:, a, :], ident_words, 2 * pair + a
+                    nc, scratch_pool, columns(name + name, b), products[:, a, :], ident_words, 2 * pair + a
                 )
 
         def spread_key_sums(b):
@@ -375,7 +371,8 @@ def tile_attention_pa_t_kernel(tc, q, k, x, Wv, out):
                         column("kk", b, T).to_broadcast([P, P]),
                         ident_words[:],
                     )
-                nc.vector.tensor_copy(
+                copy = nc.scalar.copy if b < 2 else nc.vector.tensor_copy
+                copy(
                     out=spread_rows[:, h * BANK : (h + 1) * BANK],
                     in_=spread[:].rearrange("p t c -> p (t c)"),
                 )
@@ -403,13 +400,16 @@ def tile_attention_pa_t_kernel(tc, q, k, x, Wv, out):
                 regroup_words(copy, operand[(name, b)][0], banks[(name, b, pair)], pair, name == "k")
             if 0 <= i - 1 < len(todo):
                 name, pair = todo[i - 1]
-                quantise_input_bank(name, b, pair)
-                if name == "k":
-                    multiply_keys(b, pair)
+                if pair % 2 == 1:
+                    quantise_input_banks(name, b, pair)
+                if name == "k" or (name == "q" and query_products(b)):
+                    multiply_tokens(name, b, pair)
             if 0 <= i - 2 < len(todo):
                 name, pair = todo[i - 2]
-                if name == "k":
-                    sum_key_squares(b, pair)
+                if name == "k" or (name == "q" and query_products(b)):
+                    sum_squares(name, b, pair)
+                if (name, pair) == ("q", 3) and query_products(b):
+                    scale_query_sums(b)
                 if (name, pair) == ("q", 0):
                     spread_key_sums(b)
 
@@ -417,10 +417,18 @@ def tile_attention_pa_t_kernel(tc, q, k, x, Wv, out):
             return range(-1, len(input_banks(b)) + 1)
 
         def query_square_step(b, T):
+            if query_products(b):
+                return
             square_sum(nc, scratch_pool, columns("qq", b), raw[("q", b)], T)
             if T == TILES - 1:
-                nc.vector.tensor_scalar_mul(columns("neg_qq", b), columns("qq", b), -1.0)
-                nc.vector.tensor_scalar_mul(columns("qq_over_d", b), columns("qq", b), 1.0 / D)
+                scale_query_sums(b)
+
+        def scale_query_sums(b):
+            nc.vector.tensor_scalar_mul(columns("neg_qq", b), columns("qq", b), -1.0)
+            nc.vector.tensor_scalar_mul(columns("qq_over_d", b), columns("qq", b), 1.0 / D)
+
+        def query_products(b):
+            return b == 2
 
         def score_step(b, T):
             if T + 1 < TILES:
@@ -442,12 +450,12 @@ def tile_attention_pa_t_kernel(tc, q, k, x, Wv, out):
                 value_passes(b, C)
             if C >= 1:
                 round_values(b, C - 1)
-            if C == TILES:
-                quantise_values(b)
 
         def weight_step(b, T):
             if T < TILES:
                 exponentials(b, T)
+                if T % PACK == PACK - 1:
+                    invert_sums(b, T - PACK + 1)
             if 0 <= T - 1 < TILES:
                 turn_weights(b, T - 1)
             if 0 <= T - 2 < TILES:
@@ -455,8 +463,6 @@ def tile_attention_pa_t_kernel(tc, q, k, x, Wv, out):
             if 0 <= T - 3 < TILES:
                 quantise_weights(b, T - 3)
                 weighted_sum(b, T - 3)
-                if T % 2 == 0:
-                    invert_sums(b, T - 4)
             if 0 <= T - 4 < TILES:
                 divide_and_store(b, T - 4)
 
@@ -491,6 +497,8 @@ def tile_attention_pa_t_kernel(tc, q, k, x, Wv, out):
             if 3 <= i < 3 + TILES:
                 root_step(1, i - 3)
         start_batch(3)
+        quantise_values(0)
+        quantise_values(1)
         for i in range(2 * TILES + 4):
             if i < TILES + 4:
                 weight_step(0, i)
@@ -515,6 +523,8 @@ def tile_attention_pa_t_kernel(tc, q, k, x, Wv, out):
                 value_step(3, i)
             if 3 <= i < 3 + TILES:
                 root_step(3, i - 3)
+        quantise_values(2)
+        quantise_values(3)
         for i in range(2 * TILES + 4):
             if i < TILES + 4:
                 weight_step(2, i)

@@ -110,7 +110,7 @@ def tile_attention_pa_t_kernel(tc, q, k, x, Wv, out):
         stats_pool = ctx.enter_context(tc.tile_pool(name="stats", bufs=2))
         score_pool = ctx.enter_context(tc.tile_pool(name="scores", bufs=2 * TILES))
         e_pool = ctx.enter_context(tc.tile_pool(name="e", bufs=4))
-        weight_pool = ctx.enter_context(tc.tile_pool(name="weights", bufs=3))
+        weight_pool = ctx.enter_context(tc.tile_pool(name="weights", bufs=2))
         result_pool = ctx.enter_context(tc.tile_pool(name="results", bufs=2))
         psum_staging = ctx.enter_context(tc.psum_pool(name="psum_staging", bufs=3))
         psum_sums = ctx.enter_context(tc.psum_pool(name="psum_sums", bufs=3))
@@ -118,6 +118,11 @@ def tile_attention_pa_t_kernel(tc, q, k, x, Wv, out):
 
         ident_words = const_pool.tile([P, P], F32)
         masks.make_identity(nc, ident_words[:])
+
+        one = const_pool.tile([P, 1], F32)
+        nc.vector.memset(one[:], 1.0)
+        root_of_one = const_pool.tile([P, 1], F32)
+        nc.scalar.activation(out=root_of_one[:], in_=one[:], func=ACT.Sqrt)
 
         raw = {}
         operand = {}
@@ -285,19 +290,26 @@ def tile_attention_pa_t_kernel(tc, q, k, x, Wv, out):
             banks[("e_turned", b, T)] = e_turned
 
         def group_weights(b, T):
-            e_grouped = weight_pool.tile([P, KEY_PASSES * P * PACK], BF16, tag="e_grouped", align_bytes=64)
+            values = KEY_PASSES * P * PACK
+            if T % 2 == 0:
+                two_tiles = weight_pool.tile([P, 2 * values], BF16, tag="e_grouped", align_bytes=64)
+                weights[("e_grouped", b, T // 2)] = two_tiles
+            e_grouped = weights[("e_grouped", b, T // 2)][:, T % 2 * values : (T % 2 + 1) * values]
             copy = nc.vector.tensor_copy if group_on_vector(b, T) else nc.scalar.copy
             copy(
                 out=e_grouped[:].bitcast(F32).rearrange("p (g i u) -> p g i u", g=KEY_PASSES, u=2),
                 in_=banks[("e_turned", b, T)][:].rearrange("p g u i -> p g i u"),
             )
-            weights[("e_grouped", b, T)] = e_grouped
 
         def quantise_weights(b, T):
-            e_codes = weight_pool.tile([P, KEY_PASSES * P], U32, tag="e_codes", align_bytes=64)
-            e_scales = weight_pool.tile([P, KEY_PASSES * P], U8, tag="e_scales", align_bytes=64)
-            quantise_columns(nc, e_codes, e_scales, weights[("e_grouped", b, T)], 0, KEY_PASSES * P)
-            weights[("e_codes", b, T)] = (e_codes, e_scales)
+            columns_of_tile = KEY_PASSES * P
+            e_codes = weight_pool.tile([P, 2 * columns_of_tile], U32, tag="e_codes", align_bytes=64)
+            e_scales = weight_pool.tile([P, 2 * columns_of_tile], U8, tag="e_scales", align_bytes=64)
+            two_tiles = weights[("e_grouped", b, T // 2)]
+            quantise_columns(nc, e_codes, e_scales, two_tiles, 0, 2 * columns_of_tile)
+            for a in range(2):
+                part = slice(a * columns_of_tile, (a + 1) * columns_of_tile)
+                weights[("e_codes", b, T - 1 + a)] = (e_codes[:, part], e_scales[:, part])
 
         def weighted_sum(b, T):
             e_codes, e_scales = weights[("e_codes", b, T)]
@@ -460,11 +472,12 @@ def tile_attention_pa_t_kernel(tc, q, k, x, Wv, out):
                 turn_weights(b, T - 1)
             if 0 <= T - 2 < TILES:
                 group_weights(b, T - 2)
-            if 0 <= T - 3 < TILES:
+            if 0 <= T - 3 < TILES and (T - 3) % 2 == 1:
                 quantise_weights(b, T - 3)
-                weighted_sum(b, T - 3)
             if 0 <= T - 4 < TILES:
-                divide_and_store(b, T - 4)
+                weighted_sum(b, T - 4)
+            if 0 <= T - 5 < TILES:
+                divide_and_store(b, T - 5)
 
         start_batch(0)
         wv_raw = raw_pool.tile([P, D // P, D], BF16, tag="wv_raw", bufs=1)
@@ -499,8 +512,8 @@ def tile_attention_pa_t_kernel(tc, q, k, x, Wv, out):
         start_batch(3)
         quantise_values(0)
         quantise_values(1)
-        for i in range(2 * TILES + 4):
-            if i < TILES + 4:
+        for i in range(2 * TILES + 5):
+            if i < TILES + 5:
                 weight_step(0, i)
             if i >= TILES:
                 weight_step(1, i - TILES)
@@ -525,8 +538,8 @@ def tile_attention_pa_t_kernel(tc, q, k, x, Wv, out):
                 root_step(3, i - 3)
         quantise_values(2)
         quantise_values(3)
-        for i in range(2 * TILES + 4):
-            if i < TILES + 4:
+        for i in range(2 * TILES + 5):
+            if i < TILES + 5:
                 weight_step(2, i)
             if i >= TILES:
                 weight_step(3, i - TILES)

@@ -301,15 +301,20 @@ def tile_attention_pa_t_kernel(tc, q, k, x, Wv, out):
                 in_=banks[("e_turned", b, T)][:].rearrange("p g u i -> p g i u"),
             )
 
-        def quantise_weights(b, T):
+        def quantise_weights(b, T, count):
             columns_of_tile = KEY_PASSES * P
-            e_codes = weight_pool.tile([P, 2 * columns_of_tile], U32, tag="e_codes", align_bytes=64)
-            e_scales = weight_pool.tile([P, 2 * columns_of_tile], U8, tag="e_scales", align_bytes=64)
+            if T % 2 == 0:
+                e_codes = weight_pool.tile([P, 2 * columns_of_tile], U32, tag="e_codes", align_bytes=64)
+                e_scales = weight_pool.tile([P, 2 * columns_of_tile], U8, tag="e_scales", align_bytes=64)
+                weights[("two_codes", b, T // 2)] = (e_codes, e_scales)
+            e_codes, e_scales = weights[("two_codes", b, T // 2)]
             two_tiles = weights[("e_grouped", b, T // 2)]
-            quantise_columns(nc, e_codes, e_scales, two_tiles, 0, 2 * columns_of_tile)
-            for a in range(2):
+            quantise_columns(
+                nc, e_codes, e_scales, two_tiles, T % 2 * columns_of_tile, count * columns_of_tile
+            )
+            for a in range(T % 2, T % 2 + count):
                 part = slice(a * columns_of_tile, (a + 1) * columns_of_tile)
-                weights[("e_codes", b, T - 1 + a)] = (e_codes[:, part], e_scales[:, part])
+                weights[("e_codes", b, T - T % 2 + a)] = (e_codes[:, part], e_scales[:, part])
 
         def weighted_sum(b, T):
             e_codes, e_scales = weights[("e_codes", b, T)]
@@ -472,8 +477,10 @@ def tile_attention_pa_t_kernel(tc, q, k, x, Wv, out):
                 turn_weights(b, T - 1)
             if 0 <= T - 2 < TILES:
                 group_weights(b, T - 2)
-            if 0 <= T - 3 < TILES and (T - 3) % 2 == 1:
-                quantise_weights(b, T - 3)
+            if b == B - 1 and TILES - 2 <= T - 3 < TILES:
+                quantise_weights(b, T - 3, 1)
+            elif 0 <= T - 3 < TILES and (T - 3) % 2 == 1:
+                quantise_weights(b, T - 4, 2)
             if 0 <= T - 4 < TILES:
                 weighted_sum(b, T - 4)
             if 0 <= T - 5 < TILES:

from contextlib import ExitStack

import concourse.masks as masks
import concourse.mybir as mybir

FP8X4 = mybir.dt.float8_e4m3fn_x4
BF16 = mybir.dt.bfloat16
F32 = mybir.dt.float32
U32 = mybir.dt.uint32
U8 = mybir.dt.uint8
ACT = mybir.ActivationFunctionType
ALU = mybir.AluOpType

B, N, D = 4, 1024, 512
P = 128
PACK = 4
K_PASS = P * PACK
TILES = N // P
KEY_PASSES = N // K_PASS
BANK = 512
HALVES = N // BANK

RUN = {"k": 2, "q": 4, "x": 2}

FLOPS = 2 * B * N * D * D + 2 * 2 * B * N * N * D


def load_tokens(nc, raw, rows, run, in_parts):
    tiles = raw[:].rearrange("p (g t) d -> p g t d", t=run)
    rows = rows.rearrange("(g p t) d -> p g t d", p=P, t=run)
    if in_parts:
        for g in range(TILES // run):
            nc.sync.dma_start(out=tiles[:, g], in_=rows[:, g])
    else:
        nc.sync.dma_start(out=tiles, in_=rows)


def turn_words(nc, turned, raw, pair, ident_words):
    for a in range(2):
        words = raw[:, 2 * pair + a, :].bitcast(F32)
        for u in range(2):
            nc.tensor.transpose(
                turned[:, u, a * P : (a + 1) * P], words[:, u * P : (u + 1) * P], ident_words[:]
            )


def regroup_words(copy, grouped, turned, pair, alternate_tiles):
    words = grouped[:].bitcast(F32)[:, pair * 4 * P : (pair + 1) * 4 * P]
    if alternate_tiles:
        copy(
            out=words.rearrange("p (c a u) -> p c a u", a=2, u=2),
            in_=turned[:].rearrange("p u (a c) -> p c a u", a=2),
        )
    else:
        copy(
            out=words.rearrange("p (c u) -> p c u", u=2),
            in_=turned[:].rearrange("p u c -> p c u"),
        )


def quantise_columns(nc, codes, scales, grouped, first, count):
    nc.vector.quantize_mx(
        out=codes[:, first : first + count].bitcast(FP8X4),
        scales=scales[:, first : first + count],
        in_=grouped[:, first * PACK : (first + count) * PACK],
    )


def token_products(nc, products, grouped, T):
    values = grouped[:, T * P * PACK : (T + 1) * P * PACK]
    for t in range(PACK):
        nc.tensor.matmul(
            products,
            lhsT=values[:, t :: PACK],
            rhs=values[:, t :: PACK],
            start=(t == 0),
            stop=(t == PACK - 1),
        )


def square_sum(nc, scratch_pool, sums, raw, T):
    squares = scratch_pool.tile([P, D], BF16, tag="squares")
    nc.scalar.activation(
        out=squares[:], in_=raw[:, T, :], func=ACT.Square, accum_out=sums[:, T : T + 1]
    )


def diagonal_sum(nc, scratch_pool, sums, products, ident_words, T):
    diagonal = scratch_pool.tile([P, P], F32, tag="diagonal")
    nc.vector.scalar_tensor_tensor(
        out=diagonal[:],
        in0=products,
        scalar=1.0,
        in1=ident_words[:],
        op0=ALU.mult,
        op1=ALU.mult,
        accum_out=sums[:, T : T + 1],
    )


def tile_attention_pa_t_kernel(tc, q, k, x, Wv, out):
    nc = tc.nc
    inputs = {"k": k, "q": q, "x": x}
    with ExitStack() as ctx:
        const_pool = ctx.enter_context(tc.tile_pool(name="const", bufs=1))
        raw_pool = ctx.enter_context(tc.tile_pool(name="raw", bufs=2))
        grouped_pool = ctx.enter_context(tc.tile_pool(name="grouped", bufs=3))
        operand_pool = ctx.enter_context(tc.tile_pool(name="operands", bufs=2))
        scratch_pool = ctx.enter_context(tc.tile_pool(name="scratch", bufs=2))
        stats_pool = ctx.enter_context(tc.tile_pool(name="stats", bufs=2))
        score_pool = ctx.enter_context(tc.tile_pool(name="scores", bufs=2 * TILES))
        e_pool = ctx.enter_context(tc.tile_pool(name="e", bufs=4))
        weight_pool = ctx.enter_context(tc.tile_pool(name="weights", bufs=2))
        result_pool = ctx.enter_context(tc.tile_pool(name="results", bufs=2))
        psum_staging = ctx.enter_context(tc.psum_pool(name="psum_staging", bufs=3))
        psum_sums = ctx.enter_context(tc.psum_pool(name="psum_sums", bufs=3))
        psum_turned = ctx.enter_context(tc.psum_pool(name="psum_turned", bufs=2))

        ident_words = const_pool.tile([P, P], F32)
        masks.make_identity(nc, ident_words[:])

        one = const_pool.tile([P, 1], F32)
        nc.vector.memset(one[:], 1.0)
        root_of_one = const_pool.tile([P, 1], F32)
        nc.scalar.activation(out=root_of_one[:], in_=one[:], func=ACT.Sqrt)

        raw = {}
        operand = {}
        kk_rows = {}
        stat = {}
        banks = {}
        rows = {}
        weights = {}
        results = {}

        def start_batch(b):
            if b % 2 == 0:
                for name in ("kk", "qq", "neg_qq", "qq_over_d", "peak", "row_sum", "one_over_sum"):
                    new_stat(name, b)
            for name in ("k", "q", "x"):
                rows_in = raw_pool.tile([P, TILES, D], BF16, tag=name + "_raw")
                load_tokens(nc, rows_in, inputs[name][b], RUN[name], b == 0)
                raw[(name, b)] = rows_in

        def new_operand(name, b, columns):
            grouped = grouped_pool.tile([P, columns * PACK], BF16, tag="grouped", align_bytes=64)
            codes = operand_pool.tile([P, columns], U32, tag=name + "_codes", align_bytes=64)
            scales = operand_pool.tile([P, columns], U8, tag=name + "_scales", align_bytes=64)
            operand[(name, b)] = (grouped, codes, scales)

        def new_stat(name, b):
            column_per_tile = stats_pool.tile([P, 2 * TILES], F32, tag=name)
            stat[(name, b // 2)] = column_per_tile
            return column_per_tile

        def column(name, b, T):
            place = b % 2 * TILES + T
            return stat[(name, b // 2)][:, place : place + 1]

        def columns(name, b):
            place = b % 2 * TILES
            return stat[(name, b // 2)][:, place : place + TILES]


        def regroup_on_vector(b, i):
            return b >= 2 or b == 0 and i % 4 == 0

        def group_on_vector(b, T):
            return b >= B - 2

        def divide_on_vector(b, T):
            return b >= B - 2 and T % 4 != 3


        def score_passes(b, T):
            q_codes, q_scales = operand[("q", b)][1:]
            k_codes, k_scales = operand[("k", b)][1:]
            for h in range(HALVES):
                qk = psum_sums.tile([P, BANK], F32, tag="sums")
                nc.tensor.matmul_mx(
                    out=qk[:],
                    lhsT=q_codes[:, T * P : (T + 1) * P].bitcast(FP8X4),
                    lhsT_scale=q_scales[:, T * P : (T + 1) * P],
                    rhs=k_codes[:, h * BANK : (h + 1) * BANK].bitcast(FP8X4),
                    rhs_scale=k_scales[:, h * BANK : (h + 1) * BANK],
                    start=True,
                    stop=True,
                )
                banks[("qk", b, T, h)] = qk

        def keys_minus_products(b, T):
            s = score_pool.tile([P, N], F32, tag="s")
            for h in range(HALVES):
                nc.vector.scalar_tensor_tensor(
                    out=s[:, h * BANK : (h + 1) * BANK],
                    in0=banks[("qk", b, T, h)][:],
                    scalar=-2.0,
                    in1=kk_rows[b][:, h * BANK : (h + 1) * BANK],
                    op0=ALU.mult,
                    op1=ALU.add,
                )
            rows[(b, T)] = s

        def clamp_and_peak(b, T):
            nc.vector.tensor_scalar(
                out=rows[(b, T)][:],
                in0=rows[(b, T)][:],
                scalar1=column("neg_qq", b, T),
                scalar2=None,
                op0=ALU.max,
                op1=ALU.max,
                accum_out=column("peak", b, T),
            )

        def square_root(b, T):
            nc.scalar.activation(
                out=rows[(b, T)][:],
                in_=rows[(b, T)][:],
                func=ACT.Sqrt,
                bias=column("qq_over_d", b, T),
                scale=1.0 / D,
            )

        def row_maxima(b):
            largest_d2 = new_stat("largest_d2", b)
            nc.vector.tensor_tensor(
                out=largest_d2[:], in0=stat[("peak", b // 2)][:], in1=stat[("qq", b // 2)][:], op=ALU.add
            )
            row_max = new_stat("row_max", b)
            nc.scalar.activation(out=row_max[:], in_=largest_d2[:], func=ACT.Sqrt, scale=1.0 / D)
            nc.scalar.mul(new_stat("neg_row_max", b)[:], row_max[:], -1.0)

        def value_passes(b, C):
            x_codes, x_scales = operand[("x", b)][1:]
            wv_codes, wv_scales = operand[("wv", 0)][1:]
            g, c = divmod(C, D // P)
            values = psum_turned.tile([P, PACK, P], F32, tag="e_turned")
            for t in range(PACK):
                T = g * PACK + t
                nc.tensor.matmul_mx(
                    out=values[:, t, :],
                    lhsT=x_codes[:, T * P : (T + 1) * P].bitcast(FP8X4),
                    lhsT_scale=x_scales[:, T * P : (T + 1) * P],
                    rhs=wv_codes[:, c * P : (c + 1) * P].bitcast(FP8X4),
                    rhs_scale=wv_scales[:, c * P : (c + 1) * P],
                    start=True,
                    stop=True,
                )
            banks[("values", b, C)] = values

        def round_values(b, C):
            v_grouped = operand[("v", b)][0]
            nc.scalar.copy(
                out=v_grouped[:, C * P * PACK : (C + 1) * P * PACK].rearrange("p (d t) -> p d t", t=PACK),
                in_=banks[("values", b, C)][:].rearrange("p t d -> p d t"),
            )

        def quantise_values(b):
            v_grouped, v_codes, v_scales = operand[("v", b)]
            quantise_columns(nc, v_codes, v_scales, v_grouped, 0, KEY_PASSES * D)


        def exponentials(b, T):
            e = e_pool.tile([P, N], BF16, tag="e")
            nc.scalar.activation(
                out=e[:],
                in_=rows[(b, T)][:],
                func=ACT.Exp,
                bias=column("neg_row_max", b, T),
                scale=1.0,
                accum_out=column("row_sum", b, T),
            )
            weights[("e", b, T)] = e

        def invert_sums(b, T):
            nc.vector.reciprocal(
                columns("one_over_sum", b)[:, T : T + PACK], columns("row_sum", b)[:, T : T + PACK]
            )

        def turn_weights(b, T):
            words = weights[("e", b, T)][:].bitcast(F32)
            e_turned = psum_turned.tile([P, KEY_PASSES, 2, P], F32, tag="e_turned")
            for g in range(KEY_PASSES):
                for u in range(2):
                    nc.tensor.transpose(
                        e_turned[:, g, u, :],
                        words[:, (2 * g + u) * P : (2 * g + u + 1) * P],
                        ident_words[:],
                    )
            banks[("e_turned", b, T)] = e_turned

        def group_weights(b, T):
            values = KEY_PASSES * P * PACK
            if T % 2 == 0:
                two_tiles = weight_pool.tile([P, 2 * values], BF16, tag="e_grouped", align_bytes=64)
                weights[("e_grouped", b, T // 2)] = two_tiles
            e_grouped = weights[("e_grouped", b, T // 2)][:, T % 2 * values : (T % 2 + 1) * values]
            copy = nc.vector.tensor_copy if group_on_vector(b, T) else nc.scalar.copy
            copy(
                out=e_grouped[:].bitcast(F32).rearrange("p (g i u) -> p g i u", g=KEY_PASSES, u=2),
                in_=banks[("e_turned", b, T)][:].rearrange("p g u i -> p g i u"),
            )

        def quantise_weights(b, T, count):
            columns_of_tile = KEY_PASSES * P
            if T % 2 == 0:
                e_codes = weight_pool.tile([P, 2 * columns_of_tile], U32, tag="e_codes", align_bytes=64)
                e_scales = weight_pool.tile([P, 2 * columns_of_tile], U8, tag="e_scales", align_bytes=64)
                weights[("two_codes", b, T // 2)] = (e_codes, e_scales)
            e_codes, e_scales = weights[("two_codes", b, T // 2)]
            two_tiles = weights[("e_grouped", b, T // 2)]
            quantise_columns(
                nc, e_codes, e_scales, two_tiles, T % 2 * columns_of_tile, count * columns_of_tile
            )
            for a in range(T % 2, T % 2 + count):
                part = slice(a * columns_of_tile, (a + 1) * columns_of_tile)
                weights[("e_codes", b, T - T % 2 + a)] = (e_codes[:, part], e_scales[:, part])

        def weighted_sum(b, T):
            e_codes, e_scales = weights[("e_codes", b, T)]
            v_codes, v_scales = operand[("v", b)][1:]
            summed = psum_staging.tile([P, D], F32, tag="staging")
            for g in range(KEY_PASSES):
                nc.tensor.matmul_mx(
                    out=summed[:],
                    lhsT=e_codes[:, g * P : (g + 1) * P].bitcast(FP8X4),
                    lhsT_scale=e_scales[:, g * P : (g + 1) * P],
                    rhs=v_codes[:, g * D : (g + 1) * D].bitcast(FP8X4),
                    rhs_scale=v_scales[:, g * D : (g + 1) * D],
                    start=(g == 0),
                    stop=(g == KEY_PASSES - 1),
                )
            banks[("summed", b, T)] = summed

        def divide_and_store(b, T):
            g, t = divmod(T, PACK)
            if t == 0:
                four_tiles = result_pool.tile([P, PACK, D], F32, tag="result")
                results[(b, g)] = four_tiles
            one_over_sum = column("one_over_sum", b, T)
            if divide_on_vector(b, T):
                nc.vector.tensor_scalar_mul(
                    results[(b, g)][:, t, :], banks[("summed", b, T)][:], one_over_sum
                )
            else:
                nc.scalar.activation(
                    out=results[(b, g)][:, t, :],
                    in_=banks[("summed", b, T)][:],
                    func=ACT.Copy,
                    scale=one_over_sum,
                )
            out_tiles = out[b].rearrange("(g p t) d -> p g t d", p=P, t=PACK)
            if (b, g) == (B - 1, TILES // PACK - 1):
                nc.sync.dma_start(out=out_tiles[:, g, t], in_=results[(b, g)][:, t])
            elif t == PACK - 1:
                nc.sync.dma_start(out=out_tiles[:, g], in_=results[(b, g)][:])

        def turn_input_bank(name, b, pair):
            turned = psum_staging.tile([P, 2, 2 * P], F32, tag="staging")
            turn_words(nc, turned, raw[(name, b)], pair, ident_words)
            banks[(name, b, pair)] = turned

        def quantise_input_banks(name, b, pair):
            grouped, codes, scales = operand[(name, b)]
            quantise_columns(nc, codes, scales, grouped, (pair - 1) * 2 * P, 4 * P)

        def multiply_tokens(name, b, pair):
            products = psum_sums.tile([P, 2, P], F32, tag="sums")
            for a in range(2):
                token_products(nc, products[:, a, :], operand[(name, b)][0], 2 * pair + a)
            banks[("products", name, b, pair)] = products

        def sum_squares(name, b, pair):
            products = banks[("products", name, b, pair)]
            for a in range(2):
                diagonal_sum(
                    nc, scratch_pool, columns(name + name, b), products[:, a, :], ident_words, 2 * pair + a
                )

        def spread_key_sums(b):
            spread_rows = operand_pool.tile([P, N], F32, tag="kk_rows")
            for h in range(HALVES):
                spread = psum_staging.tile([P, PACK, P], F32, tag="staging")
                for t in range(PACK):
                    T = h * PACK + t
                    nc.tensor.transpose(
                        spread[:, t, :],
                        column("kk", b, T).to_broadcast([P, P]),
                        ident_words[:],
                    )
                copy = nc.scalar.copy if b < 2 else nc.vector.tensor_copy
                copy(
                    out=spread_rows[:, h * BANK : (h + 1) * BANK],
                    in_=spread[:].rearrange("p t c -> p (t c)"),
                )
            kk_rows[b] = spread_rows


        def input_banks(b):
            names = ("k", "q", "x", "wv") if b == 0 else ("k", "q", "x")
            banks_in_order = []
            for name in names:
                tokens = D if name == "wv" else N
                banks_in_order.extend([(name, pair) for pair in range(tokens // (2 * P))])
            return banks_in_order

        def operand_step(b, i):
            todo = input_banks(b)
            if i + 1 < len(todo):
                name, pair = todo[i + 1]
                if pair == 0:
                    new_operand(name, b, D if name == "wv" else N)
                turn_input_bank(name, b, pair)
            if 0 <= i < len(todo):
                name, pair = todo[i]
                copy = nc.vector.tensor_copy if regroup_on_vector(b, i) else nc.scalar.copy
                regroup_words(copy, operand[(name, b)][0], banks[(name, b, pair)], pair, name == "k")
            if 0 <= i - 1 < len(todo):
                name, pair = todo[i - 1]
                if pair % 2 == 1:
                    quantise_input_banks(name, b, pair)
                if name == "k" or (name == "q" and query_products(b)):
                    multiply_tokens(name, b, pair)
            if 0 <= i - 2 < len(todo):
                name, pair = todo[i - 2]
                if name == "k" or (name == "q" and query_products(b)):
                    sum_squares(name, b, pair)
                if (name, pair) == ("q", 3) and query_products(b):
                    scale_query_sums(b)
                if (name, pair) == ("q", 0):
                    spread_key_sums(b)

        def operand_steps(b):
            return range(-1, len(input_banks(b)) + 1)

        def query_square_step(b, T):
            if query_products(b):
                return
            square_sum(nc, scratch_pool, columns("qq", b), raw[("q", b)], T)
            if T == TILES - 1:
                scale_query_sums(b)

        def scale_query_sums(b):
            nc.vector.tensor_scalar_mul(columns("neg_qq", b), columns("qq", b), -1.0)
            nc.vector.tensor_scalar_mul(columns("qq_over_d", b), columns("qq", b), 1.0 / D)

        def query_products(b):
            return b == 2

        def score_step(b, T):
            if T + 1 < TILES:
                score_passes(b, T + 1)
            if 0 <= T < TILES:
                keys_minus_products(b, T)
            if 0 <= T - 1 < TILES:
                clamp_and_peak(b, T - 1)

        def root_step(b, T):
            square_root(b, T)
            if b % 2 == 1 and T == TILES - 1:
                row_maxima(b)

        def value_step(b, C):
            if C == 0:
                new_operand("v", b, KEY_PASSES * D)
            if C < TILES:
                value_passes(b, C)
            if C >= 1:
                round_values(b, C - 1)

        def weight_step(b, T):
            if T < TILES:
                exponentials(b, T)
                if T % PACK == PACK - 1:
                    invert_sums(b, T - PACK + 1)
            if 0 <= T - 1 < TILES:
                turn_weights(b, T - 1)
            if 0 <= T - 2 < TILES:
                group_weights(b, T - 2)
            if b == B - 1 and TILES - 2 <= T - 3 < TILES:
                quantise_weights(b, T - 3, 1)
            elif 0 <= T - 3 < TILES and (T - 3) % 2 == 1:
                quantise_weights(b, T - 4, 2)
            if 0 <= T - 4 < TILES:
                weighted_sum(b, T - 4)
            if 0 <= T - 5 < TILES:
                divide_and_store(b, T - 5)

        start_batch(0)
        wv_raw = raw_pool.tile([P, D // P, D], BF16, tag="wv_raw", bufs=1)
        nc.sync.dma_start(out=wv_raw[:], in_=Wv.rearrange("(t p) f -> p t f", p=P))
        raw[("wv", 0)] = wv_raw
        start_batch(1)
        for i in operand_steps(0):
            operand_step(0, i)
            if i >= 1 and i - 1 < TILES:
                query_square_step(0, i - 1)
        start_batch(2)
        for i in range(13):
            if i - 1 <= TILES:
                score_step(0, i - 1)
            operand_step(1, i - 1)
            if i < TILES:
                query_square_step(1, i)
            if 3 <= i < 3 + TILES:
                root_step(0, i - 3)
            if i < TILES + 1:
                value_step(0, i)
        operand_step(1, 12)
        for i in range(13):
            if i - 1 <= TILES:
                score_step(1, i - 1)
            if i < TILES:
                query_square_step(2, i)
            if i < TILES + 1:
                value_step(1, i)
            if 3 <= i < 3 + TILES:
                root_step(1, i - 3)
        start_batch(3)
        quantise_values(0)
        quantise_values(1)
        for i in range(2 * TILES + 5):
            if i < TILES + 5:
                weight_step(0, i)
            if i >= TILES:
                weight_step(1, i - TILES)
            if i < 7:
                for n in (2 * i - 1, 2 * i):
                    operand_step(2, n)
            elif i - 7 - 1 <= TILES:
                score_step(2, i - 7 - 1)
        for i in range(14):
            operand_step(3, i - 1)
            if i < TILES:
                query_square_step(3, i)
                root_step(2, i)
            if 4 <= i < 4 + TILES + 1:
                value_step(2, i - 4)
        for i in range(13):
            if i - 1 <= TILES:
                score_step(3, i - 1)
            if i < TILES + 1:
                value_step(3, i)
            if 3 <= i < 3 + TILES:
                root_step(3, i - 3)
        quantise_values(2)
        quantise_values(3)
        for i in range(2 * TILES + 5):
            if i < TILES + 5:
                weight_step(2, i)
            if i >= TILES:
                weight_step(3, i - TILES)
